import numpy as np
import ml_dtypes


def mxq(x, axis, fmt="e4m3"):
    dtype, down = {"e4m3": (ml_dtypes.float8_e4m3fn, 7), "e5m2": (ml_dtypes.float8_e5m2, 14)}[fmt]
    v = np.moveaxis(np.asarray(x, np.float32).astype(ml_dtypes.bfloat16).astype(np.float64), axis, -1)
    blocks = v.reshape(v.shape[:-1] + (-1, 32))
    amax = np.abs(blocks).max(-1, keepdims=True)
    byte = np.maximum(np.where(amax > 0, np.frexp(amax)[1] - 1 + 127, 0) - down, 1)
    scale = np.exp2(byte - 127.0)
    codes = (blocks / scale).astype(np.float32).astype(dtype).astype(np.float64)
    return np.moveaxis((codes * scale).reshape(v.shape), -1, axis)


WIDE = False


def mx_kscale(k):
    if not WIDE:
        return np.ones(k)
    levels = np.array([10, -10, 5, -5, 0])
    a = np.random.permutation(np.resize(levels, k // 512 * 4)).reshape(k // 512, 4)
    idx = np.arange(k)
    return np.exp2(a[idx // 512, idx % 128 // 32])


BF16 = ml_dtypes.bfloat16


def bf(x):
    return np.asarray(x, np.float32).astype(BF16)


def f64(x):
    return np.asarray(x).astype(np.float64)


M, N, C = 8192, 512, 512
ALPHA = 0.1
BETA = np.log(0.5 / 4 + 1)


def setup_inputs():
    s = mx_kscale(N)
    limit = np.sqrt(6.0 / (C + C))
    return {"x": bf(np.random.standard_normal((N, C)) / s[:, None]),
            "x_0": bf(np.random.standard_normal((M, C))),
            "adj": bf(np.random.uniform(0.0, 1.0, (M, N)) * np.sqrt(3.0 / N) * s),
            "weight1": bf(np.random.uniform(-limit, limit, (C, C)))}


def reference(x, x_0, adj, weight1):
    h = mxq(f64(adj), 1, "e4m3") @ mxq(f64(x), 0, "e4m3")
    out = (1.0 - ALPHA) * h + ALPHA * f64(x_0)
    return (1.0 - BETA) * out + BETA * (mxq(out, 1, "e4m3") @ mxq(f64(weight1), 0, "e4m3"))

@@ -1,0 +1,225 @@
+from contextlib import ExitStack
+
+import concourse.mybir as mybir
+from concourse.masks import make_identity
+
+F32 = mybir.dt.float32
+BF16 = mybir.dt.bfloat16
+U32 = mybir.dt.uint32
+U8 = mybir.dt.uint8
+FP8X4 = mybir.dt.float8_e4m3fn_x4
+ALU = mybir.AluOpType
+ACT = mybir.ActivationFunctionType
+
+P = 128
+M_ROWS, K_IN, C_OUT = 8192, 512, 512
+FLOPS = 2 * 2 * M_ROWS * K_IN * C_OUT
+
+BETA = 0.11778303565638346
+C_H = (1.0 - BETA) * 0.9
+C_X0 = (1.0 - BETA) * 0.1
+INV = 1.0 / (1.0 - BETA)
+
+CHUNK = 512
+N_CHUNKS = M_ROWS // CHUNK
+N_UNITS = 2 * N_CHUNKS
+AHEAD = 6
+
+
+def tile_gcnlayer_pa_t_kernel(tc, x, x_0, adj, weight1, out):
+    nc = tc.nc
+    with ExitStack() as ctx:
+        const = ctx.enter_context(tc.tile_pool(name="const", bufs=1))
+        inp = ctx.enter_context(tc.tile_pool(name="inp", bufs=AHEAD))
+        mid = ctx.enter_context(tc.tile_pool(name="mid", bufs=2))
+        res = ctx.enter_context(tc.tile_pool(name="res", bufs=6))
+        ps_a = ctx.enter_context(tc.psum_pool(name="ps_a", bufs=1))
+        ps_h = ctx.enter_context(tc.psum_pool(name="ps_h", bufs=2))
+        ps_t = ctx.enter_context(tc.psum_pool(name="ps_t", bufs=2))
+        ps_p = ctx.enter_context(tc.psum_pool(name="ps_p", bufs=3))
+        ctx.enter_context(tc.manual_schedule())
+
+        adj_t, x0_t, x0s_t, s_t = {}, {}, {}, {}
+        ga_t, ca_t, sa_t = {}, {}, {}
+        gm_t, cm_t, sm_t = {}, {}, {}
+        pa_t, ph_t, pt_t, pp_t = {}, {}, {}, {}
+
+        def load(g):
+            rows = slice(g * CHUNK, (g + 1) * CHUNK)
+            a = inp.tile([P, 2048], BF16, name="adj_sb", tag="adj_sb")
+            nc.sync.dma_start(out=a[:], in_=adj[rows, :].rearrange("(p t) k -> p (t k)", t=4))
+            adj_t[g] = a
+            b = inp.tile([P, 2048], BF16, name="x0_sb", tag="x0_sb")
+            nc.sync.dma_start(out=b[:], in_=x_0[rows, :].rearrange("(p t) k -> p (t k)", t=4))
+            x0_t[g] = b
+
+        def weight_load(view, label, split):
+            raw = const.tile([P, 4, 512], BF16, name="raw_" + label, tag="raw_" + label)
+            if split:
+                nc.sync.dma_start(out=raw[:].rearrange("p (u e) c -> p u e c", u=2), in_=view)
+            else:
+                nc.sync.dma_start(out=raw[:], in_=view)
+            return raw
+
+        def weight_quantise(raw, label):
+            grouped = const.tile([P, 2048], BF16, name="grp_" + label, tag="grp_" + label, align_bytes=64)
+            nc.vector.tensor_copy(
+                out=grouped[:].rearrange("p (c j) -> p c j", j=4),
+                in_=raw[:].rearrange("p j c -> p c j"),
+            )
+            codes = const.tile([P, 512], U32, name="cod_" + label, tag="cod_" + label, align_bytes=64)
+            scales = const.tile([P, 512], U8, name="scl_" + label, tag="scl_" + label, align_bytes=64)
+            nc.vector.quantize_mx(out=codes[:].bitcast(FP8X4), scales=scales[:], in_=grouped[:])
+            return codes, scales
+
+        def stage_x0(u):
+            g, h = divmod(u, 2)
+            if h == 0:
+                x0s = mid.tile([P, 2048], F32, name="x0s", tag="x0s", bufs=3)
+                x0s_t[g] = x0s
+            cols = slice(1024 * h, 1024 * h + 1024)
+            nc.gpsimd.tensor_scalar(
+                out=x0s_t[g][:, cols], in0=x0_t[g][:, cols],
+                scalar1=C_X0, scalar2=0.0, op0=ALU.mult, op1=ALU.add,
+            )
+
+        def stage_a(u):
+            g, h = divmod(u, 2)
+            pa = ps_a.tile([P, 512], F32, name="pa", tag="pa")
+            words = adj_t[g][:].bitcast(F32)
+            for i in range(4):
+                src = 512 * h + 128 * i
+                nc.tensor.transpose(pa[:, 128 * i:128 * i + 128], words[:, src:src + 128], ident[:])
+            pa_t[u] = pa
+
+        def stage_sa(u):
+            g, h = divmod(u, 2)
+            if h == 0:
+                ga = mid.tile([P, 2048], BF16, name="ga", tag="ga", align_bytes=64)
+                ga_t[g] = ga
+            gw = ga_t[g][:].bitcast(F32)
+            nc.scalar.copy(
+                out=gw[:, 512 * h:512 * h + 512].rearrange("p (t r u) -> p t r u", t=2, u=2),
+                in_=pa_t[u][:].rearrange("p (t u r) -> p t r u", t=2, u=2),
+            )
+
+        def stage_q(u, grouped_t, codes_t, scales_t, label):
+            g, h = divmod(u, 2)
+            if h == 0:
+                codes = mid.tile([P, 512], U32, name="c" + label, tag="c" + label, align_bytes=64)
+                scales = mid.tile([P, 512], U8, name="s" + label, tag="s" + label, align_bytes=64)
+                codes_t[g] = codes
+                scales_t[g] = scales
+            nc.vector.quantize_mx(
+                out=codes_t[g][:, 256 * h:256 * h + 256].bitcast(FP8X4),
+                scales=scales_t[g][:, 256 * h:256 * h + 256],
+                in_=grouped_t[g][:, 1024 * h:1024 * h + 1024],
+            )
+
+        def stage_mx(u, pool, label, codes_t, scales_t, w_codes, w_scales, bank_t):
+            g, h = divmod(u, 2)
+            for i in range(2):
+                t = 2 * h + i
+                bank = pool.tile([P, 512], F32, name=label, tag=label)
+                nc.tensor.matmul_mx(
+                    out=bank[:],
+                    lhsT=codes_t[g][:, 128 * t:128 * t + 128].bitcast(FP8X4),
+                    lhsT_scale=scales_t[g][:, 128 * t:128 * t + 128],
+                    rhs=w_codes[:].bitcast(FP8X4),
+                    rhs_scale=w_scales[:],
+                    start=True,
+                    stop=True,
+                )
+                bank_t[(u, i)] = bank
+
+        def stage_c1(u):
+            g, h = divmod(u, 2)
+            if h == 0:
+                s = res.tile([P, 2048], F32, name="s_sb", tag="s_sb")
+                s_t[g] = s
+            for i in range(2):
+                cols = slice(1024 * h + 512 * i, 1024 * h + 512 * i + 512)
+                nc.vector.scalar_tensor_tensor(
+                    out=s_t[g][:, cols], in0=ph_t[(u, i)][:], scalar=C_H, in1=x0s_t[g][:, cols],
+                    op0=ALU.mult, op1=ALU.add,
+                )
+
+        def stage_t(u):
+            g, h = divmod(u, 2)
+            for i in range(2):
+                pt = ps_t.tile([P, 512], F32, name="pt", tag="pt")
+                base = 1024 * h + 512 * i
+                for j in range(4):
+                    nc.tensor.transpose(
+                        pt[:, 128 * j:128 * j + 128], s_t[g][:, base + 128 * j:base + 128 * j + 128], ident[:]
+                    )
+                pt_t[(u, i)] = pt
+
+        def stage_st(u):
+            g, h = divmod(u, 2)
+            if h == 0:
+                gm = mid.tile([P, 2048], BF16, name="gm", tag="gm", align_bytes=64)
+                gm_t[g] = gm
+            for i in range(2):
+                base = 1024 * h + 512 * i
+                nc.scalar.activation(
+                    out=gm_t[g][:, base:base + 512].rearrange("p (r j) -> p r j", j=4),
+                    in_=pt_t[(u, i)][:].rearrange("p (j r) -> p r j", j=4),
+                    func=ACT.Copy,
+                    scale=INV,
+                )
+
+        def stage_c2(u):
+            g, h = divmod(u, 2)
+            for i in range(2):
+                cols = slice(1024 * h + 512 * i, 1024 * h + 512 * i + 512)
+                nc.vector.scalar_tensor_tensor(
+                    out=s_t[g][:, cols], in0=pp_t[(u, i)][:], scalar=BETA, in1=s_t[g][:, cols],
+                    op0=ALU.mult, op1=ALU.add,
+                )
+            view = out[g * CHUNK:(g + 1) * CHUNK, :].rearrange("(p t) c -> p t c", t=4)
+            nc.sync.dma_start(
+                out=view[:, 2 * h:2 * h + 2, :],
+                in_=s_t[g][:, 1024 * h:1024 * h + 1024].rearrange("p (t c) -> p t c", t=2),
+            )
+
+        ident = const.tile([P, P], F32, name="ident", tag="ident")
+        make_identity(nc, ident[:])
+
+        rows0 = slice(0, CHUNK)
+        a0 = inp.tile([P, 2048], BF16, name="adj_sb", tag="adj_sb")
+        nc.sync.dma_start(out=a0[:], in_=adj[rows0, :].rearrange("(p t) k -> p (t k)", t=4))
+        adj_t[0] = a0
+        x_raw = weight_load(x.rearrange("(u w e) c -> w u e c", u=2, e=2), "x", True)
+        b0 = inp.tile([P, 2048], BF16, name="x0_sb", tag="x0_sb")
+        nc.sync.dma_start(out=b0[:], in_=x_0[rows0, :].rearrange("(p t) k -> p (t k)", t=4))
+        x0_t[0] = b0
+        w_raw = weight_load(weight1.rearrange("(j p) n -> p j n", p=P), "w", False)
+        for g in range(1, AHEAD):
+            load(g)
+
+        x_codes, x_scales = weight_quantise(x_raw, "x")
+        w_q = {}
+
+        for n in range(N_UNITS + 4):
+            if n < N_UNITS:
+                stage_x0(n)
+                stage_a(n)
+                stage_sa(n)
+                stage_q(n, ga_t, ca_t, sa_t, "a")
+            if n == 1:
+                w_q["c"], w_q["s"] = weight_quantise(w_raw, "w")
+            if 0 <= n - 3 < N_UNITS:
+                stage_t(n - 3)
+                stage_st(n - 3)
+            if 0 <= n - 1 < N_UNITS:
+                stage_mx(n - 1, ps_h, "ph", ca_t, sa_t, x_codes, x_scales, ph_t)
+                stage_c1(n - 1)
+            if 0 <= n - 4 < N_UNITS:
+                stage_mx(n - 4, ps_p, "pp", cm_t, sm_t, w_q["c"], w_q["s"], pp_t)
+                stage_c2(n - 4)
+                g_done, h_done = divmod(n - 4, 2)
+                if h_done == 1 and g_done + AHEAD < N_CHUNKS:
+                    load(g_done + AHEAD)
+            if 0 <= n - 3 < N_UNITS:
+                stage_q(n - 3, gm_t, cm_t, sm_t, "m")

@@ -74,14 +74,18 @@ def tile_gcnlayer_pa_t_kernel(tc, x, x_0, adj, weight1, out):
 
         def stage_x0(u):
             g, h = divmod(u, 2)
-            if h == 0:
-                x0s = mid.tile([P, 2048], F32, name="x0s", tag="x0s", bufs=3)
-                x0s_t[g] = x0s
-            cols = slice(1024 * h, 1024 * h + 1024)
-            nc.gpsimd.tensor_scalar(
-                out=x0s_t[g][:, cols], in0=x0_t[g][:, cols],
-                scalar1=C_X0, scalar2=0.0, op0=ALU.mult, op1=ALU.add,
-            )
+            for i in range(2):
+                cols = slice(1024 * h + 512 * i, 1024 * h + 512 * i + 512)
+                if i == 0:
+                    x0s = mid.tile([P, 512], F32, name="x0s_g", tag="x0s_g")
+                    nc.gpsimd.tensor_scalar(
+                        out=x0s[:], in0=x0_t[g][:, cols],
+                        scalar1=C_X0, scalar2=0.0, op0=ALU.mult, op1=ALU.add,
+                    )
+                else:
+                    x0s = mid.tile([P, 512], F32, name="x0s_s", tag="x0s_s", bufs=3)
+                    nc.scalar.activation(out=x0s[:], in_=x0_t[g][:, cols], func=ACT.Copy, scale=C_X0)
+                x0s_t[(u, i)] = x0s
 
         def stage_a(u):
             g, h = divmod(u, 2)
@@ -140,7 +144,7 @@ def tile_gcnlayer_pa_t_kernel(tc, x, x_0, adj, weight1, out):
             for i in range(2):
                 cols = slice(1024 * h + 512 * i, 1024 * h + 512 * i + 512)
                 nc.vector.scalar_tensor_tensor(
-                    out=s_t[g][:, cols], in0=ph_t[(u, i)][:], scalar=C_H, in1=x0s_t[g][:, cols],
+                    out=s_t[g][:, cols], in0=ph_t[(u, i)][:], scalar=C_H, in1=x0s_t[(u, i)][:],
                     op0=ALU.mult, op1=ALU.add,
                 )
 
@@ -203,18 +207,22 @@ def tile_gcnlayer_pa_t_kernel(tc, x, x_0, adj, weight1, out):
 
         for n in range(N_UNITS + 4):
             if n < N_UNITS:
-                stage_x0(n)
                 stage_a(n)
                 stage_sa(n)
                 stage_q(n, ga_t, ca_t, sa_t, "a")
+            if n == 0:
+                stage_x0(0)
+                stage_x0(1)
             if n == 1:
                 w_q["c"], w_q["s"] = weight_quantise(w_raw, "w")
-            if 0 <= n - 3 < N_UNITS:
-                stage_t(n - 3)
-                stage_st(n - 3)
             if 0 <= n - 1 < N_UNITS:
                 stage_mx(n - 1, ps_h, "ph", ca_t, sa_t, x_codes, x_scales, ph_t)
                 stage_c1(n - 1)
+                if n + 1 < N_UNITS:
+                    stage_x0(n + 1)
+            if 0 <= n - 3 < N_UNITS:
+                stage_t(n - 3)
+                stage_st(n - 3)
             if 0 <= n - 4 < N_UNITS:
                 stage_mx(n - 4, ps_p, "pp", cm_t, sm_t, w_q["c"], w_q["s"], pp_t)
                 stage_c2(n - 4)

@@ -31,7 +31,7 @@ def tile_gcnlayer_pa_t_kernel(tc, x, x_0, adj, weight1, out):
     with ExitStack() as ctx:
         const = ctx.enter_context(tc.tile_pool(name="const", bufs=1))
         inp = ctx.enter_context(tc.tile_pool(name="inp", bufs=AHEAD))
-        mid = ctx.enter_context(tc.tile_pool(name="mid", bufs=2))
+        mid = ctx.enter_context(tc.tile_pool(name="mid", bufs=3))
         res = ctx.enter_context(tc.tile_pool(name="res", bufs=6))
         ps_a = ctx.enter_context(tc.psum_pool(name="ps_a", bufs=1))
         ps_h = ctx.enter_context(tc.psum_pool(name="ps_h", bufs=2))
@@ -39,37 +39,43 @@ def tile_gcnlayer_pa_t_kernel(tc, x, x_0, adj, weight1, out):
         ps_p = ctx.enter_context(tc.psum_pool(name="ps_p", bufs=3))
         ctx.enter_context(tc.manual_schedule())
 
-        adj_t, x0_t, x0s_t, s_t = {}, {}, {}, {}
+        adj_t, x0_t, x0s_t, s_t, ev_t = {}, {}, {}, {}, {}
         ga_t, ca_t, sa_t = {}, {}, {}
         gm_t, cm_t, sm_t = {}, {}, {}
         pa_t, ph_t, pt_t, pp_t = {}, {}, {}, {}
 
-        def load(g):
-            rows = slice(g * CHUNK, (g + 1) * CHUNK)
+        def load_adj(g):
             a = inp.tile([P, 2048], BF16, name="adj_sb", tag="adj_sb")
-            nc.sync.dma_start(out=a[:], in_=adj[rows, :].rearrange("(p t) k -> p (t k)", t=4))
+            nc.sync.dma_start(out=a[:], in_=adj[g * CHUNK:(g + 1) * CHUNK, :].rearrange("(p t) k -> p (t k)", t=4))
             adj_t[g] = a
+
+        def load_x0(g):
             b = inp.tile([P, 2048], BF16, name="x0_sb", tag="x0_sb")
-            nc.sync.dma_start(out=b[:], in_=x_0[rows, :].rearrange("(p t) k -> p (t k)", t=4))
+            nc.sync.dma_start(out=b[:], in_=x_0[g * CHUNK:(g + 1) * CHUNK, :].rearrange("(p t) k -> p (t k)", t=4))
             x0_t[g] = b
 
-        def weight_load(view, label, split):
-            raw = const.tile([P, 4, 512], BF16, name="raw_" + label, tag="raw_" + label)
-            if split:
-                nc.sync.dma_start(out=raw[:].rearrange("p (u e) c -> p u e c", u=2), in_=view)
-            else:
-                nc.sync.dma_start(out=raw[:], in_=view)
-            return raw
-
-        def weight_quantise(raw, label):
+        def weight_regroup(raw, label, on_gpsimd):
             grouped = const.tile([P, 2048], BF16, name="grp_" + label, tag="grp_" + label, align_bytes=64)
-            nc.vector.tensor_copy(
-                out=grouped[:].rearrange("p (c j) -> p c j", j=4),
-                in_=raw[:].rearrange("p j c -> p c j"),
-            )
+            dst = grouped[:].rearrange("p (c j) -> p c j", j=4)
+            src = raw[:].rearrange("p j c -> p c j")
+            if on_gpsimd:
+                nc.gpsimd.tensor_scalar(out=dst, in0=src, scalar1=1.0, scalar2=0.0, op0=ALU.mult, op1=ALU.add)
+            else:
+                nc.vector.tensor_copy(out=dst, in_=src)
+            return grouped
+
+        def weight_quantise(grouped, label):
             codes = const.tile([P, 512], U32, name="cod_" + label, tag="cod_" + label, align_bytes=64)
             scales = const.tile([P, 512], U8, name="scl_" + label, tag="scl_" + label, align_bytes=64)
             nc.vector.quantize_mx(out=codes[:].bitcast(FP8X4), scales=scales[:], in_=grouped[:])
+            return codes, scales
+
+        def quantise(grouped, lo, hi, label):
+            codes = mid.tile([P, 512], U32, name="c" + label, tag="c" + label, align_bytes=64)
+            scales = mid.tile([P, 512], U8, name="s" + label, tag="s" + label, align_bytes=64)
+            nc.vector.quantize_mx(
+                out=codes[:, lo // 4:hi // 4].bitcast(FP8X4), scales=scales[:, lo // 4:hi // 4], in_=grouped[:, lo:hi]
+            )
             return codes, scales
 
         def stage_x0(u):
@@ -77,13 +83,12 @@ def tile_gcnlayer_pa_t_kernel(tc, x, x_0, adj, weight1, out):
             for i in range(2):
                 cols = slice(1024 * h + 512 * i, 1024 * h + 512 * i + 512)
                 if i == 0:
-                    x0s = mid.tile([P, 512], F32, name="x0s_g", tag="x0s_g")
+                    x0s = mid.tile([P, 512], F32, name="x0s_g", tag="x0s_g", bufs=2)
                     nc.gpsimd.tensor_scalar(
-                        out=x0s[:], in0=x0_t[g][:, cols],
-                        scalar1=C_X0, scalar2=0.0, op0=ALU.mult, op1=ALU.add,
+                        out=x0s[:], in0=x0_t[g][:, cols], scalar1=C_X0, scalar2=0.0, op0=ALU.mult, op1=ALU.add
                     )
                 else:
-                    x0s = mid.tile([P, 512], F32, name="x0s_s", tag="x0s_s", bufs=3)
+                    x0s = mid.tile([P, 512], F32, name="x0s_s", tag="x0s_s")
                     nc.scalar.activation(out=x0s[:], in_=x0_t[g][:, cols], func=ACT.Copy, scale=C_X0)
                 x0s_t[(u, i)] = x0s
 
@@ -94,50 +99,29 @@ def tile_gcnlayer_pa_t_kernel(tc, x, x_0, adj, weight1, out):
             for i in range(4):
                 src = 512 * h + 128 * i
                 nc.tensor.transpose(pa[:, 128 * i:128 * i + 128], words[:, src:src + 128], ident[:])
-            pa_t[u] = pa
-
-        def stage_sa(u):
-            g, h = divmod(u, 2)
             if h == 0:
                 ga = mid.tile([P, 2048], BF16, name="ga", tag="ga", align_bytes=64)
                 ga_t[g] = ga
             gw = ga_t[g][:].bitcast(F32)
             nc.scalar.copy(
                 out=gw[:, 512 * h:512 * h + 512].rearrange("p (t r u) -> p t r u", t=2, u=2),
-                in_=pa_t[u][:].rearrange("p (t u r) -> p t r u", t=2, u=2),
+                in_=pa[:].rearrange("p (t u r) -> p t r u", t=2, u=2),
             )
 
-        def stage_q(u, grouped_t, codes_t, scales_t, label):
-            g, h = divmod(u, 2)
-            if h == 0:
-                codes = mid.tile([P, 512], U32, name="c" + label, tag="c" + label, align_bytes=64)
-                scales = mid.tile([P, 512], U8, name="s" + label, tag="s" + label, align_bytes=64)
-                codes_t[g] = codes
-                scales_t[g] = scales
-            nc.vector.quantize_mx(
-                out=codes_t[g][:, 256 * h:256 * h + 256].bitcast(FP8X4),
-                scales=scales_t[g][:, 256 * h:256 * h + 256],
-                in_=grouped_t[g][:, 1024 * h:1024 * h + 1024],
+        def mx_pass(pool, label, codes, scales, col, w_codes, w_scales):
+            bank = pool.tile([P, 512], F32, name=label, tag=label)
+            nc.tensor.matmul_mx(
+                out=bank[:],
+                lhsT=codes[:, col:col + 128].bitcast(FP8X4), lhsT_scale=scales[:, col:col + 128],
+                rhs=w_codes[:].bitcast(FP8X4), rhs_scale=w_scales[:],
+                start=True, stop=True,
             )
+            return bank
 
-        def stage_mx(u, pool, label, codes_t, scales_t, w_codes, w_scales, bank_t):
+        def stage_h(u):
             g, h = divmod(u, 2)
             for i in range(2):
-                t = 2 * h + i
-                bank = pool.tile([P, 512], F32, name=label, tag=label)
-                nc.tensor.matmul_mx(
-                    out=bank[:],
-                    lhsT=codes_t[g][:, 128 * t:128 * t + 128].bitcast(FP8X4),
-                    lhsT_scale=scales_t[g][:, 128 * t:128 * t + 128],
-                    rhs=w_codes[:].bitcast(FP8X4),
-                    rhs_scale=w_scales[:],
-                    start=True,
-                    stop=True,
-                )
-                bank_t[(u, i)] = bank
-
-        def stage_c1(u):
-            g, h = divmod(u, 2)
+                ph_t[(u, i)] = mx_pass(ps_h, "ph", ca_t[g], sa_t[g], 256 * h + 128 * i, x_codes, x_scales)
             if h == 0:
                 s = res.tile([P, 2048], F32, name="s_sb", tag="s_sb")
                 s_t[g] = s
@@ -150,6 +134,7 @@ def tile_gcnlayer_pa_t_kernel(tc, x, x_0, adj, weight1, out):
 
         def stage_t(u):
             g, h = divmod(u, 2)
+            mc, pos = divmod(u + 1, 2)
             for i in range(2):
                 pt = ps_t.tile([P, 512], F32, name="pt", tag="pt")
                 base = 1024 * h + 512 * i
@@ -158,76 +143,101 @@ def tile_gcnlayer_pa_t_kernel(tc, x, x_0, adj, weight1, out):
                         pt[:, 128 * j:128 * j + 128], s_t[g][:, base + 128 * j:base + 128 * j + 128], ident[:]
                     )
                 pt_t[(u, i)] = pt
-
-        def stage_st(u):
-            g, h = divmod(u, 2)
-            if h == 0:
+            if mc not in gm_t:
                 gm = mid.tile([P, 2048], BF16, name="gm", tag="gm", align_bytes=64)
-                gm_t[g] = gm
+                gm_t[mc] = gm
             for i in range(2):
-                base = 1024 * h + 512 * i
+                base = 1024 * pos + 512 * i
                 nc.scalar.activation(
-                    out=gm_t[g][:, base:base + 512].rearrange("p (r j) -> p r j", j=4),
+                    out=gm_t[mc][:, base:base + 512].rearrange("p (r j) -> p r j", j=4),
                     in_=pt_t[(u, i)][:].rearrange("p (j r) -> p r j", j=4),
-                    func=ACT.Copy,
-                    scale=INV,
+                    func=ACT.Copy, scale=INV,
                 )
 
-        def stage_c2(u):
+        def store(u):
             g, h = divmod(u, 2)
-            for i in range(2):
-                cols = slice(1024 * h + 512 * i, 1024 * h + 512 * i + 512)
-                nc.vector.scalar_tensor_tensor(
-                    out=s_t[g][:, cols], in0=pp_t[(u, i)][:], scalar=BETA, in1=s_t[g][:, cols],
-                    op0=ALU.mult, op1=ALU.add,
-                )
             view = out[g * CHUNK:(g + 1) * CHUNK, :].rearrange("(p t) c -> p t c", t=4)
             nc.sync.dma_start(
                 out=view[:, 2 * h:2 * h + 2, :],
                 in_=s_t[g][:, 1024 * h:1024 * h + 1024].rearrange("p (t c) -> p t c", t=2),
             )
 
+        def stage_p(u):
+            g, h = divmod(u, 2)
+            mc, pos = divmod(u + 1, 2)
+            for i in range(2):
+                pp_t[(u, i)] = mx_pass(ps_p, "pp", cm_t[mc], sm_t[mc], 256 * pos + 128 * i, w_q["c"], w_q["s"])
+            for i in range(2):
+                cols = slice(1024 * h + 512 * i, 1024 * h + 512 * i + 512)
+                if i == 1 and u % 2 == 0:
+                    ev = mid.tile([P, 512], F32, name="ev", tag="ev", bufs=2)
+                    nc.scalar.activation(out=ev[:], in_=pp_t[(u, i)][:], func=ACT.Copy, scale=BETA)
+                    ev_t[u] = ev
+                else:
+                    nc.vector.scalar_tensor_tensor(
+                        out=s_t[g][:, cols], in0=pp_t[(u, i)][:], scalar=BETA, in1=s_t[g][:, cols],
+                        op0=ALU.mult, op1=ALU.add,
+                    )
+            if u % 2 == 1:
+                store(u)
+
+        def stage_add(u):
+            g, h = divmod(u, 2)
+            cols = slice(1024 * h + 512, 1024 * h + 1024)
+            nc.gpsimd.tensor_tensor(out=s_t[g][:, cols], in0=ev_t[u][:], in1=s_t[g][:, cols], op=ALU.add)
+            store(u)
+
         ident = const.tile([P, P], F32, name="ident", tag="ident")
         make_identity(nc, ident[:])
 
-        rows0 = slice(0, CHUNK)
-        a0 = inp.tile([P, 2048], BF16, name="adj_sb", tag="adj_sb")
-        nc.sync.dma_start(out=a0[:], in_=adj[rows0, :].rearrange("(p t) k -> p (t k)", t=4))
-        adj_t[0] = a0
-        x_raw = weight_load(x.rearrange("(u w e) c -> w u e c", u=2, e=2), "x", True)
-        b0 = inp.tile([P, 2048], BF16, name="x0_sb", tag="x0_sb")
-        nc.sync.dma_start(out=b0[:], in_=x_0[rows0, :].rearrange("(p t) k -> p (t k)", t=4))
-        x0_t[0] = b0
-        w_raw = weight_load(weight1.rearrange("(j p) n -> p j n", p=P), "w", False)
-        for g in range(1, AHEAD):
-            load(g)
+        load_adj(0)
+        x_raw = const.tile([P, 4, 512], BF16, name="x_raw", tag="x_raw")
+        nc.sync.dma_start(
+            out=x_raw[:].rearrange("p (u e) c -> p u e c", u=2), in_=x.rearrange("(u w e) c -> w u e c", u=2, e=2)
+        )
+        load_x0(0)
+        w_raw = const.tile([P, 4, 512], BF16, name="w_raw", tag="w_raw")
+        nc.sync.dma_start(out=w_raw[:], in_=weight1.rearrange("(j p) n -> p j n", p=P))
+        load_adj(1)
+        load_x0(1)
+        for g in range(2, AHEAD):
+            load_adj(g)
+            load_x0(g)
 
-        x_codes, x_scales = weight_quantise(x_raw, "x")
+        x_codes, x_scales = weight_quantise(weight_regroup(x_raw, "x", False), "x")
         w_q = {}
 
-        for n in range(N_UNITS + 4):
-            if n < N_UNITS:
-                stage_a(n)
-                stage_sa(n)
-                stage_q(n, ga_t, ca_t, sa_t, "a")
-            if n == 0:
+        def live(u):
+            return 0 <= u < N_UNITS
+
+        for j in range(-5, N_UNITS + 4):
+            if j % 2 == 0:
+                mc = j // 2 - 1
+                lo = 0 if live(j - 3) else 1024
+                hi = 2048 if live(j - 2) else 1024
+                if lo < hi:
+                    cm_t[mc], sm_t[mc] = quantise(gm_t[mc], lo, hi, "m")
+                g_next = j // 2 + 1
+                if 0 <= g_next < N_CHUNKS:
+                    ca_t[g_next], sa_t[g_next] = quantise(ga_t[g_next], 0, 2048, "a")
+            if j == -1:
                 stage_x0(0)
                 stage_x0(1)
-            if n == 1:
-                w_q["c"], w_q["s"] = weight_quantise(w_raw, "w")
-            if 0 <= n - 1 < N_UNITS:
-                stage_mx(n - 1, ps_h, "ph", ca_t, sa_t, x_codes, x_scales, ph_t)
-                stage_c1(n - 1)
-                if n + 1 < N_UNITS:
-                    stage_x0(n + 1)
-            if 0 <= n - 3 < N_UNITS:
-                stage_t(n - 3)
-                stage_st(n - 3)
-            if 0 <= n - 4 < N_UNITS:
-                stage_mx(n - 4, ps_p, "pp", cm_t, sm_t, w_q["c"], w_q["s"], pp_t)
-                stage_c2(n - 4)
-                g_done, h_done = divmod(n - 4, 2)
-                if h_done == 1 and g_done + AHEAD < N_CHUNKS:
-                    load(g_done + AHEAD)
-            if 0 <= n - 3 < N_UNITS:
-                stage_q(n - 3, gm_t, cm_t, sm_t, "m")
+                w_q["g"] = weight_regroup(w_raw, "w", True)
+            if live(j):
+                stage_h(j)
+                if j == 1:
+                    w_q["c"], w_q["s"] = weight_quantise(w_q["g"], "w")
+                if live(j + 2):
+                    stage_x0(j + 2)
+            if j % 2 == 0 and live(j - 4):
+                stage_add(j - 4)
+            if live(j - 1):
+                stage_t(j - 1)
+            if live(j - 3):
+                stage_p(j - 3)
+            if live(j + 5):
+                stage_a(j + 5)
+            if j >= 0 and j % 2 == 0 and j // 2 + AHEAD < N_CHUNKS:
+                load_adj(j // 2 + AHEAD)
+                load_x0(j // 2 + AHEAD)

@@ -78,19 +78,18 @@ def tile_gcnlayer_pa_t_kernel(tc, x, x_0, adj, weight1, out):
             )
             return codes, scales
 
-        def stage_x0(u):
+        def prep_x0(u, i, on_gpsimd):
             g, h = divmod(u, 2)
-            for i in range(2):
-                cols = slice(1024 * h + 512 * i, 1024 * h + 512 * i + 512)
-                if i == 0:
-                    x0s = mid.tile([P, 512], F32, name="x0s_g", tag="x0s_g", bufs=2)
-                    nc.gpsimd.tensor_scalar(
-                        out=x0s[:], in0=x0_t[g][:, cols], scalar1=C_X0, scalar2=0.0, op0=ALU.mult, op1=ALU.add
-                    )
-                else:
-                    x0s = mid.tile([P, 512], F32, name="x0s_s", tag="x0s_s")
-                    nc.scalar.activation(out=x0s[:], in_=x0_t[g][:, cols], func=ACT.Copy, scale=C_X0)
-                x0s_t[(u, i)] = x0s
+            cols = slice(1024 * h + 512 * i, 1024 * h + 512 * i + 512)
+            if on_gpsimd:
+                x0s = mid.tile([P, 512], F32, name="x0s_g%d" % i, tag="x0s_g%d" % i, bufs=2)
+                nc.gpsimd.tensor_scalar(
+                    out=x0s[:], in0=x0_t[g][:, cols], scalar1=C_X0, scalar2=0.0, op0=ALU.mult, op1=ALU.add
+                )
+            else:
+                x0s = mid.tile([P, 512], F32, name="x0s_s", tag="x0s_s", bufs=2)
+                nc.scalar.activation(out=x0s[:], in_=x0_t[g][:, cols], func=ACT.Copy, scale=C_X0)
+            x0s_t[(u, i)] = x0s
 
         def stage_a(u):
             g, h = divmod(u, 2)
@@ -221,23 +220,29 @@ def tile_gcnlayer_pa_t_kernel(tc, x, x_0, adj, weight1, out):
                 if 0 <= g_next < N_CHUNKS:
                     ca_t[g_next], sa_t[g_next] = quantise(ga_t[g_next], 0, 2048, "a")
             if j == -1:
-                stage_x0(0)
-                stage_x0(1)
+                prep_x0(0, 0, True)
+                prep_x0(0, 1, False)
+                prep_x0(1, 0, True)
+                prep_x0(1, 1, True)
                 w_q["g"] = weight_regroup(w_raw, "w", True)
             if live(j):
                 stage_h(j)
                 if j == 1:
                     w_q["c"], w_q["s"] = weight_quantise(w_q["g"], "w")
                 if live(j + 2):
-                    stage_x0(j + 2)
+                    prep_x0(j + 2, 0, True)
             if j % 2 == 0 and live(j - 4):
                 stage_add(j - 4)
-            if live(j - 1):
-                stage_t(j - 1)
+            if j >= 0 and j % 2 == 0 and live(j + 3):
+                prep_x0(j + 3, 1, True)
             if live(j - 3):
                 stage_p(j - 3)
+            if live(j - 1):
+                stage_t(j - 1)
             if live(j + 5):
                 stage_a(j + 5)
+            if j >= 0 and j % 2 == 0 and live(j + 2):
+                prep_x0(j + 2, 1, False)
             if j >= 0 and j % 2 == 0 and j // 2 + AHEAD < N_CHUNKS:
                 load_adj(j // 2 + AHEAD)
                 load_x0(j // 2 + AHEAD)

@@ -235,10 +235,10 @@ def tile_gcnlayer_pa_t_kernel(tc, x, x_0, adj, weight1, out):
                 stage_add(j - 4)
             if j >= 0 and j % 2 == 0 and live(j + 3):
                 prep_x0(j + 3, 1, True)
-            if live(j - 3):
-                stage_p(j - 3)
             if live(j - 1):
                 stage_t(j - 1)
+            if live(j - 3):
+                stage_p(j - 3)
             if live(j + 5):
                 stage_a(j + 5)
             if j >= 0 and j % 2 == 0 and live(j + 2):

@@ -32,7 +32,7 @@ def tile_gcnlayer_pa_t_kernel(tc, x, x_0, adj, weight1, out):
         const = ctx.enter_context(tc.tile_pool(name="const", bufs=1))
         inp = ctx.enter_context(tc.tile_pool(name="inp", bufs=AHEAD))
         mid = ctx.enter_context(tc.tile_pool(name="mid", bufs=3))
-        res = ctx.enter_context(tc.tile_pool(name="res", bufs=6))
+        res = ctx.enter_context(tc.tile_pool(name="res", bufs=7))
         ps_a = ctx.enter_context(tc.psum_pool(name="ps_a", bufs=1))
         ps_h = ctx.enter_context(tc.psum_pool(name="ps_h", bufs=2))
         ps_t = ctx.enter_context(tc.psum_pool(name="ps_t", bufs=2))
@@ -133,7 +133,7 @@ def tile_gcnlayer_pa_t_kernel(tc, x, x_0, adj, weight1, out):
 
         def stage_t(u):
             g, h = divmod(u, 2)
-            mc, pos = divmod(u + 1, 2)
+            mc, pos = divmod(u, 2)
             for i in range(2):
                 pt = ps_t.tile([P, 512], F32, name="pt", tag="pt")
                 base = 1024 * h + 512 * i
@@ -163,7 +163,7 @@ def tile_gcnlayer_pa_t_kernel(tc, x, x_0, adj, weight1, out):
 
         def stage_p(u):
             g, h = divmod(u, 2)
-            mc, pos = divmod(u + 1, 2)
+            mc, pos = divmod(u, 2)
             for i in range(2):
                 pp_t[(u, i)] = mx_pass(ps_p, "pp", cm_t[mc], sm_t[mc], 256 * pos + 128 * i, w_q["c"], w_q["s"])
             for i in range(2):
@@ -209,13 +209,11 @@ def tile_gcnlayer_pa_t_kernel(tc, x, x_0, adj, weight1, out):
         def live(u):
             return 0 <= u < N_UNITS
 
-        for j in range(-5, N_UNITS + 4):
+        for j in range(-5, N_UNITS + 5):
             if j % 2 == 0:
-                mc = j // 2 - 1
-                lo = 0 if live(j - 3) else 1024
-                hi = 2048 if live(j - 2) else 1024
-                if lo < hi:
-                    cm_t[mc], sm_t[mc] = quantise(gm_t[mc], lo, hi, "m")
+                mc = j // 2 - 2
+                if 0 <= mc < N_CHUNKS:
+                    cm_t[mc], sm_t[mc] = quantise(gm_t[mc], 0, 2048, "m")
                 g_next = j // 2 + 1
                 if 0 <= g_next < N_CHUNKS:
                     ca_t[g_next], sa_t[g_next] = quantise(ga_t[g_next], 0, 2048, "a")
@@ -231,14 +229,14 @@ def tile_gcnlayer_pa_t_kernel(tc, x, x_0, adj, weight1, out):
                     w_q["c"], w_q["s"] = weight_quantise(w_q["g"], "w")
                 if live(j + 2):
                     prep_x0(j + 2, 0, True)
-            if j % 2 == 0 and live(j - 4):
-                stage_add(j - 4)
+            if j % 2 == 0 and live(j - 6):
+                stage_add(j - 6)
             if j >= 0 and j % 2 == 0 and live(j + 3):
                 prep_x0(j + 3, 1, True)
+            if live(j - 5):
+                stage_p(j - 5)
             if live(j - 1):
                 stage_t(j - 1)
-            if live(j - 3):
-                stage_p(j - 3)
             if live(j + 5):
                 stage_a(j + 5)
             if j >= 0 and j % 2 == 0 and live(j + 2):

@@ -12,235 +12,216 @@ ALU = mybir.AluOpType
 ACT = mybir.ActivationFunctionType
 
 P = 128
-M_ROWS, K_IN, C_OUT = 8192, 512, 512
-FLOPS = 2 * 2 * M_ROWS * K_IN * C_OUT
+ROWS, NODES, FEATS = 8192, 512, 512
+FLOPS = 2 * ROWS * NODES * FEATS + 2 * ROWS * FEATS * FEATS
 
 BETA = 0.11778303565638346
 C_H = (1.0 - BETA) * 0.9
 C_X0 = (1.0 - BETA) * 0.1
-INV = 1.0 / (1.0 - BETA)
+UNDO = 1.0 / (1.0 - BETA)
 
-CHUNK = 512
-N_CHUNKS = M_ROWS // CHUNK
+TILE_COLS = 512
+UNIT_COLS = 2 * TILE_COLS
+CHUNK_COLS = 2 * UNIT_COLS
+CHUNK_ROWS = 4 * P
+N_CHUNKS = ROWS // CHUNK_ROWS
 N_UNITS = 2 * N_CHUNKS
-AHEAD = 6
+
+A_LEAD = 5
+X0_LEAD = 2
+T_LAG = 1
+P_LAG = 5
+ADD_LAG = 6
+LOADS_AHEAD = 6
 
 
 def tile_gcnlayer_pa_t_kernel(tc, x, x_0, adj, weight1, out):
     nc = tc.nc
     with ExitStack() as ctx:
         const = ctx.enter_context(tc.tile_pool(name="const", bufs=1))
-        inp = ctx.enter_context(tc.tile_pool(name="inp", bufs=AHEAD))
-        mid = ctx.enter_context(tc.tile_pool(name="mid", bufs=3))
-        res = ctx.enter_context(tc.tile_pool(name="res", bufs=7))
-        ps_a = ctx.enter_context(tc.psum_pool(name="ps_a", bufs=1))
-        ps_h = ctx.enter_context(tc.psum_pool(name="ps_h", bufs=2))
-        ps_t = ctx.enter_context(tc.psum_pool(name="ps_t", bufs=2))
-        ps_p = ctx.enter_context(tc.psum_pool(name="ps_p", bufs=3))
+        inputs = ctx.enter_context(tc.tile_pool(name="inputs", bufs=LOADS_AHEAD))
+        stream = ctx.enter_context(tc.tile_pool(name="stream", bufs=3))
+        results = ctx.enter_context(tc.tile_pool(name="results", bufs=7))
+        bank_a = ctx.enter_context(tc.psum_pool(name="bank_a", bufs=1))
+        bank_h = ctx.enter_context(tc.psum_pool(name="bank_h", bufs=2))
+        bank_t = ctx.enter_context(tc.psum_pool(name="bank_t", bufs=2))
+        bank_p = ctx.enter_context(tc.psum_pool(name="bank_p", bufs=3))
         ctx.enter_context(tc.manual_schedule())
 
-        adj_t, x0_t, x0s_t, s_t, ev_t = {}, {}, {}, {}, {}
-        ga_t, ca_t, sa_t = {}, {}, {}
-        gm_t, cm_t, sm_t = {}, {}, {}
-        pa_t, ph_t, pt_t, pp_t = {}, {}, {}, {}
+        adj_sb, x0_sb, x0_scaled, s_sb, p_scaled = {}, {}, {}, {}, {}
+        adj_grouped, adj_codes, adj_scales = {}, {}, {}
+        m_grouped, m_codes, m_scales = {}, {}, {}
+        weights = {}
 
-        def load_adj(g):
-            a = inp.tile([P, 2048], BF16, name="adj_sb", tag="adj_sb")
-            nc.sync.dma_start(out=a[:], in_=adj[g * CHUNK:(g + 1) * CHUNK, :].rearrange("(p t) k -> p (t k)", t=4))
-            adj_t[g] = a
+        def first_col(u, i):
+            return (u % 2) * UNIT_COLS + i * TILE_COLS
 
-        def load_x0(g):
-            b = inp.tile([P, 2048], BF16, name="x0_sb", tag="x0_sb")
-            nc.sync.dma_start(out=b[:], in_=x_0[g * CHUNK:(g + 1) * CHUNK, :].rearrange("(p t) k -> p (t k)", t=4))
-            x0_t[g] = b
+        def tile_cols(u, i):
+            return slice(first_col(u, i), first_col(u, i) + TILE_COLS)
 
-        def weight_regroup(raw, label, on_gpsimd):
-            grouped = const.tile([P, 2048], BF16, name="grp_" + label, tag="grp_" + label, align_bytes=64)
-            dst = grouped[:].rearrange("p (c j) -> p c j", j=4)
-            src = raw[:].rearrange("p j c -> p c j")
-            if on_gpsimd:
+        def chunk_rows(dram, g):
+            return dram[g * CHUNK_ROWS:(g + 1) * CHUNK_ROWS, :]
+
+        def load_chunk(g):
+            adj_sb[g] = inputs.tile([P, CHUNK_COLS], BF16, name="adj_sb", tag="adj_sb")
+            nc.sync.dma_start(out=adj_sb[g][:], in_=chunk_rows(adj, g).rearrange("(p t) k -> p (t k)", t=4))
+            x0_sb[g] = inputs.tile([P, CHUNK_COLS], BF16, name="x0_sb", tag="x0_sb")
+            nc.sync.dma_start(out=x0_sb[g][:], in_=chunk_rows(x_0, g).rearrange("(p t) k -> p (t k)", t=4))
+
+        def store_unit(u):
+            rows = chunk_rows(out, u // 2).rearrange("(p t) c -> p t c", t=4)
+            first = 2 * (u % 2)
+            cols = slice((u % 2) * UNIT_COLS, (u % 2 + 1) * UNIT_COLS)
+            nc.sync.dma_start(
+                out=rows[:, first:first + 2, :], in_=s_sb[u // 2][:, cols].rearrange("p (t c) -> p t c", t=2)
+            )
+
+        def quantise(pool, grouped, label):
+            codes = pool.tile([P, CHUNK_COLS // 4], U32, name="codes_" + label, tag="codes_" + label, align_bytes=64)
+            scales = pool.tile([P, CHUNK_COLS // 4], U8, name="scales_" + label, tag="scales_" + label, align_bytes=64)
+            nc.vector.quantize_mx(out=codes[:].bitcast(FP8X4), scales=scales[:], in_=grouped[:])
+            return codes, scales
+
+        def regroup_weight(engine_is_gpsimd, raw, label):
+            grouped = const.tile([P, CHUNK_COLS], BF16, name="grouped_" + label, tag="grouped_" + label, align_bytes=64)
+            dst = grouped[:].rearrange("p (c t) -> p c t", t=4)
+            src = raw[:].rearrange("p t c -> p c t")
+            if engine_is_gpsimd:
                 nc.gpsimd.tensor_scalar(out=dst, in0=src, scalar1=1.0, scalar2=0.0, op0=ALU.mult, op1=ALU.add)
             else:
                 nc.vector.tensor_copy(out=dst, in_=src)
             return grouped
 
-        def weight_quantise(grouped, label):
-            codes = const.tile([P, 512], U32, name="cod_" + label, tag="cod_" + label, align_bytes=64)
-            scales = const.tile([P, 512], U8, name="scl_" + label, tag="scl_" + label, align_bytes=64)
-            nc.vector.quantize_mx(out=codes[:].bitcast(FP8X4), scales=scales[:], in_=grouped[:])
-            return codes, scales
-
-        def quantise(grouped, lo, hi, label):
-            codes = mid.tile([P, 512], U32, name="c" + label, tag="c" + label, align_bytes=64)
-            scales = mid.tile([P, 512], U8, name="s" + label, tag="s" + label, align_bytes=64)
-            nc.vector.quantize_mx(
-                out=codes[:, lo // 4:hi // 4].bitcast(FP8X4), scales=scales[:, lo // 4:hi // 4], in_=grouped[:, lo:hi]
+        def scale_x0(u):
+            on_gpsimd = stream.tile([P, TILE_COLS], F32, name="x0_gpsimd", tag="x0_gpsimd", bufs=2)
+            nc.gpsimd.tensor_scalar(
+                out=on_gpsimd[:], in0=x0_sb[u // 2][:, tile_cols(u, 0)],
+                scalar1=C_X0, scalar2=0.0, op0=ALU.mult, op1=ALU.add,
             )
-            return codes, scales
+            on_scalar = stream.tile([P, TILE_COLS], F32, name="x0_scalar", tag="x0_scalar")
+            nc.scalar.activation(out=on_scalar[:], in_=x0_sb[u // 2][:, tile_cols(u, 1)], func=ACT.Copy, scale=C_X0)
+            x0_scaled[u] = (on_gpsimd, on_scalar)
 
-        def prep_x0(u, i, on_gpsimd):
-            g, h = divmod(u, 2)
-            cols = slice(1024 * h + 512 * i, 1024 * h + 512 * i + 512)
-            if on_gpsimd:
-                x0s = mid.tile([P, 512], F32, name="x0s_g%d" % i, tag="x0s_g%d" % i, bufs=2)
-                nc.gpsimd.tensor_scalar(
-                    out=x0s[:], in0=x0_t[g][:, cols], scalar1=C_X0, scalar2=0.0, op0=ALU.mult, op1=ALU.add
-                )
-            else:
-                x0s = mid.tile([P, 512], F32, name="x0s_s", tag="x0s_s", bufs=2)
-                nc.scalar.activation(out=x0s[:], in_=x0_t[g][:, cols], func=ACT.Copy, scale=C_X0)
-            x0s_t[(u, i)] = x0s
-
-        def stage_a(u):
-            g, h = divmod(u, 2)
-            pa = ps_a.tile([P, 512], F32, name="pa", tag="pa")
-            words = adj_t[g][:].bitcast(F32)
+        def transpose_adj(u):
+            g, half = divmod(u, 2)
+            bank = bank_a.tile([P, 4 * P], F32, name="adj_t", tag="adj_t")
+            words = adj_sb[g][:].bitcast(F32)
             for i in range(4):
-                src = 512 * h + 128 * i
-                nc.tensor.transpose(pa[:, 128 * i:128 * i + 128], words[:, src:src + 128], ident[:])
-            if h == 0:
-                ga = mid.tile([P, 2048], BF16, name="ga", tag="ga", align_bytes=64)
-                ga_t[g] = ga
-            gw = ga_t[g][:].bitcast(F32)
+                first = half * 4 * P + i * P
+                nc.tensor.transpose(bank[:, i * P:(i + 1) * P], words[:, first:first + P], identity[:])
+            if half == 0:
+                adj_grouped[g] = stream.tile([P, CHUNK_COLS], BF16, name="adj_grouped", tag="adj_grouped", align_bytes=64)
+            grouped_words = adj_grouped[g][:].bitcast(F32)[:, half * 4 * P:(half + 1) * 4 * P]
             nc.scalar.copy(
-                out=gw[:, 512 * h:512 * h + 512].rearrange("p (t r u) -> p t r u", t=2, u=2),
-                in_=pa[:].rearrange("p (t u r) -> p t r u", t=2, u=2),
+                out=grouped_words.rearrange("p (t r v) -> p t r v", t=2, v=2),
+                in_=bank[:].rearrange("p (t v r) -> p t r v", t=2, v=2),
             )
 
-        def mx_pass(pool, label, codes, scales, col, w_codes, w_scales):
-            bank = pool.tile([P, 512], F32, name=label, tag=label)
+        def mx_product(pool, label, codes, scales, u, i, moving):
+            rows = slice(((u % 2) * 2 + i) * P, ((u % 2) * 2 + i + 1) * P)
+            bank = pool.tile([P, TILE_COLS], F32, name=label, tag=label)
             nc.tensor.matmul_mx(
                 out=bank[:],
-                lhsT=codes[:, col:col + 128].bitcast(FP8X4), lhsT_scale=scales[:, col:col + 128],
-                rhs=w_codes[:].bitcast(FP8X4), rhs_scale=w_scales[:],
+                lhsT=codes[:, rows].bitcast(FP8X4), lhsT_scale=scales[:, rows],
+                rhs=weights[moving][0][:].bitcast(FP8X4), rhs_scale=weights[moving][1][:],
                 start=True, stop=True,
             )
             return bank
 
-        def stage_h(u):
-            g, h = divmod(u, 2)
+        def first_product(u):
+            g = u // 2
+            banks = [mx_product(bank_h, "h", adj_codes[g], adj_scales[g], u, i, "x") for i in range(2)]
+            if u % 2 == 0:
+                s_sb[g] = results.tile([P, CHUNK_COLS], F32, name="s_sb", tag="s_sb")
             for i in range(2):
-                ph_t[(u, i)] = mx_pass(ps_h, "ph", ca_t[g], sa_t[g], 256 * h + 128 * i, x_codes, x_scales)
-            if h == 0:
-                s = res.tile([P, 2048], F32, name="s_sb", tag="s_sb")
-                s_t[g] = s
-            for i in range(2):
-                cols = slice(1024 * h + 512 * i, 1024 * h + 512 * i + 512)
                 nc.vector.scalar_tensor_tensor(
-                    out=s_t[g][:, cols], in0=ph_t[(u, i)][:], scalar=C_H, in1=x0s_t[(u, i)][:],
+                    out=s_sb[g][:, tile_cols(u, i)], in0=banks[i][:], scalar=C_H, in1=x0_scaled[u][i][:],
                     op0=ALU.mult, op1=ALU.add,
                 )
 
-        def stage_t(u):
-            g, h = divmod(u, 2)
-            mc, pos = divmod(u, 2)
+        def transpose_s(u):
+            g = u // 2
+            banks = []
             for i in range(2):
-                pt = ps_t.tile([P, 512], F32, name="pt", tag="pt")
-                base = 1024 * h + 512 * i
-                for j in range(4):
+                bank = bank_t.tile([P, 4 * P], F32, name="s_t", tag="s_t")
+                first = first_col(u, i)
+                for t in range(4):
                     nc.tensor.transpose(
-                        pt[:, 128 * j:128 * j + 128], s_t[g][:, base + 128 * j:base + 128 * j + 128], ident[:]
+                        bank[:, t * P:(t + 1) * P], s_sb[g][:, first + t * P:first + (t + 1) * P], identity[:]
                     )
-                pt_t[(u, i)] = pt
-            if mc not in gm_t:
-                gm = mid.tile([P, 2048], BF16, name="gm", tag="gm", align_bytes=64)
-                gm_t[mc] = gm
+                banks.append(bank)
+            if u % 2 == 0:
+                m_grouped[g] = stream.tile([P, CHUNK_COLS], BF16, name="m_grouped", tag="m_grouped", align_bytes=64)
             for i in range(2):
-                base = 1024 * pos + 512 * i
                 nc.scalar.activation(
-                    out=gm_t[mc][:, base:base + 512].rearrange("p (r j) -> p r j", j=4),
-                    in_=pt_t[(u, i)][:].rearrange("p (j r) -> p r j", j=4),
-                    func=ACT.Copy, scale=INV,
+                    out=m_grouped[g][:, tile_cols(u, i)].rearrange("p (r t) -> p r t", t=4),
+                    in_=banks[i][:].rearrange("p (t r) -> p r t", t=4),
+                    func=ACT.Copy, scale=UNDO,
                 )
 
-        def store(u):
-            g, h = divmod(u, 2)
-            view = out[g * CHUNK:(g + 1) * CHUNK, :].rearrange("(p t) c -> p t c", t=4)
-            nc.sync.dma_start(
-                out=view[:, 2 * h:2 * h + 2, :],
-                in_=s_t[g][:, 1024 * h:1024 * h + 1024].rearrange("p (t c) -> p t c", t=2),
-            )
-
-        def stage_p(u):
-            g, h = divmod(u, 2)
-            mc, pos = divmod(u, 2)
+        def second_product(u):
+            g = u // 2
+            banks = [mx_product(bank_p, "p", m_codes[g], m_scales[g], u, i, "w") for i in range(2)]
             for i in range(2):
-                pp_t[(u, i)] = mx_pass(ps_p, "pp", cm_t[mc], sm_t[mc], 256 * pos + 128 * i, w_q["c"], w_q["s"])
-            for i in range(2):
-                cols = slice(1024 * h + 512 * i, 1024 * h + 512 * i + 512)
-                if i == 1 and u % 2 == 0:
-                    ev = mid.tile([P, 512], F32, name="ev", tag="ev", bufs=2)
-                    nc.scalar.activation(out=ev[:], in_=pp_t[(u, i)][:], func=ACT.Copy, scale=BETA)
-                    ev_t[u] = ev
+                if u % 2 == 0 and i == 1:
+                    p_scaled[u] = stream.tile([P, TILE_COLS], F32, name="p_scaled", tag="p_scaled", bufs=2)
+                    nc.scalar.activation(out=p_scaled[u][:], in_=banks[i][:], func=ACT.Copy, scale=BETA)
                 else:
                     nc.vector.scalar_tensor_tensor(
-                        out=s_t[g][:, cols], in0=pp_t[(u, i)][:], scalar=BETA, in1=s_t[g][:, cols],
+                        out=s_sb[g][:, tile_cols(u, i)], in0=banks[i][:], scalar=BETA, in1=s_sb[g][:, tile_cols(u, i)],
                         op0=ALU.mult, op1=ALU.add,
                     )
             if u % 2 == 1:
-                store(u)
+                store_unit(u)
 
-        def stage_add(u):
-            g, h = divmod(u, 2)
-            cols = slice(1024 * h + 512, 1024 * h + 1024)
-            nc.gpsimd.tensor_tensor(out=s_t[g][:, cols], in0=ev_t[u][:], in1=s_t[g][:, cols], op=ALU.add)
-            store(u)
-
-        ident = const.tile([P, P], F32, name="ident", tag="ident")
-        make_identity(nc, ident[:])
-
-        load_adj(0)
-        x_raw = const.tile([P, 4, 512], BF16, name="x_raw", tag="x_raw")
-        nc.sync.dma_start(
-            out=x_raw[:].rearrange("p (u e) c -> p u e c", u=2), in_=x.rearrange("(u w e) c -> w u e c", u=2, e=2)
-        )
-        load_x0(0)
-        w_raw = const.tile([P, 4, 512], BF16, name="w_raw", tag="w_raw")
-        nc.sync.dma_start(out=w_raw[:], in_=weight1.rearrange("(j p) n -> p j n", p=P))
-        load_adj(1)
-        load_x0(1)
-        for g in range(2, AHEAD):
-            load_adj(g)
-            load_x0(g)
-
-        x_codes, x_scales = weight_quantise(weight_regroup(x_raw, "x", False), "x")
-        w_q = {}
+        def finish_on_gpsimd(u):
+            cols = tile_cols(u, 1)
+            nc.gpsimd.tensor_tensor(out=s_sb[u // 2][:, cols], in0=p_scaled[u][:], in1=s_sb[u // 2][:, cols], op=ALU.add)
+            store_unit(u)
 
         def live(u):
             return 0 <= u < N_UNITS
 
-        for j in range(-5, N_UNITS + 5):
+        identity = const.tile([P, P], F32, name="identity", tag="identity")
+        make_identity(nc, identity[:])
+
+        adj_sb[0] = inputs.tile([P, CHUNK_COLS], BF16, name="adj_sb", tag="adj_sb")
+        nc.sync.dma_start(out=adj_sb[0][:], in_=chunk_rows(adj, 0).rearrange("(p t) k -> p (t k)", t=4))
+        x_raw = const.tile([P, 4, FEATS], BF16, name="x_raw", tag="x_raw")
+        nc.sync.dma_start(
+            out=x_raw[:].rearrange("p (u e) c -> p u e c", u=2), in_=x.rearrange("(u p e) c -> p u e c", u=2, e=2)
+        )
+        x0_sb[0] = inputs.tile([P, CHUNK_COLS], BF16, name="x0_sb", tag="x0_sb")
+        nc.sync.dma_start(out=x0_sb[0][:], in_=chunk_rows(x_0, 0).rearrange("(p t) k -> p (t k)", t=4))
+        w_raw = const.tile([P, 4, FEATS], BF16, name="w_raw", tag="w_raw")
+        nc.sync.dma_start(out=w_raw[:], in_=weight1.rearrange("(t p) c -> p t c", p=P))
+        for g in range(1, LOADS_AHEAD):
+            load_chunk(g)
+
+        weights["x"] = quantise(const, regroup_weight(False, x_raw, "x"), "x")
+
+        for j in range(-A_LEAD, N_UNITS + ADD_LAG - 1):
             if j % 2 == 0:
-                mc = j // 2 - 2
-                if 0 <= mc < N_CHUNKS:
-                    cm_t[mc], sm_t[mc] = quantise(gm_t[mc], 0, 2048, "m")
-                g_next = j // 2 + 1
-                if 0 <= g_next < N_CHUNKS:
-                    ca_t[g_next], sa_t[g_next] = quantise(ga_t[g_next], 0, 2048, "a")
-            if j == -1:
-                prep_x0(0, 0, True)
-                prep_x0(0, 1, False)
-                prep_x0(1, 0, True)
-                prep_x0(1, 1, True)
-                w_q["g"] = weight_regroup(w_raw, "w", True)
+                g_m, g_adj = j // 2 - 2, j // 2 + 1
+                if 0 <= g_m < N_CHUNKS:
+                    m_codes[g_m], m_scales[g_m] = quantise(stream, m_grouped[g_m], "m")
+                if 0 <= g_adj < N_CHUNKS:
+                    adj_codes[g_adj], adj_scales[g_adj] = quantise(stream, adj_grouped[g_adj], "adj")
             if live(j):
-                stage_h(j)
-                if j == 1:
-                    w_q["c"], w_q["s"] = weight_quantise(w_q["g"], "w")
-                if live(j + 2):
-                    prep_x0(j + 2, 0, True)
-            if j % 2 == 0 and live(j - 6):
-                stage_add(j - 6)
-            if j >= 0 and j % 2 == 0 and live(j + 3):
-                prep_x0(j + 3, 1, True)
-            if live(j - 5):
-                stage_p(j - 5)
-            if live(j - 1):
-                stage_t(j - 1)
-            if live(j + 5):
-                stage_a(j + 5)
-            if j >= 0 and j % 2 == 0 and live(j + 2):
-                prep_x0(j + 2, 1, False)
-            if j >= 0 and j % 2 == 0 and j // 2 + AHEAD < N_CHUNKS:
-                load_adj(j // 2 + AHEAD)
-                load_x0(j // 2 + AHEAD)
+                first_product(j)
+            if live(j + X0_LEAD):
+                scale_x0(j + X0_LEAD)
+            if j == -1:
+                w_grouped = regroup_weight(True, w_raw, "w")
+            if j == 1:
+                weights["w"] = quantise(const, w_grouped, "w")
+            if j % 2 == 0 and live(j - ADD_LAG):
+                finish_on_gpsimd(j - ADD_LAG)
+            if live(j - P_LAG):
+                second_product(j - P_LAG)
+            if live(j - T_LAG):
+                transpose_s(j - T_LAG)
+            if live(j + A_LEAD):
+                transpose_adj(j + A_LEAD)
+            if j >= 0 and j % 2 == 0 and j // 2 + LOADS_AHEAD < N_CHUNKS:
+                load_chunk(j // 2 + LOADS_AHEAD)

@@ -26,12 +26,6 @@ CHUNK_COLS = 2 * UNIT_COLS
 CHUNK_ROWS = 4 * P
 N_CHUNKS = ROWS // CHUNK_ROWS
 N_UNITS = 2 * N_CHUNKS
-
-A_LEAD = 5
-X0_LEAD = 2
-T_LAG = 1
-P_LAG = 5
-ADD_LAG = 6
 LOADS_AHEAD = 6
 
 
@@ -49,179 +43,213 @@ def tile_gcnlayer_pa_t_kernel(tc, x, x_0, adj, weight1, out):
         ctx.enter_context(tc.manual_schedule())
 
         adj_sb, x0_sb, x0_scaled, s_sb, p_scaled = {}, {}, {}, {}, {}
-        adj_grouped, adj_codes, adj_scales = {}, {}, {}
-        m_grouped, m_codes, m_scales = {}, {}, {}
+        adj_bank, adj_grouped, adj_mx = {}, {}, {}
+        s_bank, m_grouped, m_mx = {}, {}, {}
+        h_bank, p_bank = {}, {}
         weights = {}
 
-        def first_col(u, i):
-            return (u % 2) * UNIT_COLS + i * TILE_COLS
-
         def tile_cols(u, i):
-            return slice(first_col(u, i), first_col(u, i) + TILE_COLS)
+            first = (u % 2) * UNIT_COLS + i * TILE_COLS
+            return slice(first, first + TILE_COLS)
 
         def chunk_rows(dram, g):
-            return dram[g * CHUNK_ROWS:(g + 1) * CHUNK_ROWS, :]
+            return dram[g * CHUNK_ROWS:(g + 1) * CHUNK_ROWS, :].rearrange("(p t) k -> p t k", t=4)
 
-        def load_chunk(g):
-            adj_sb[g] = inputs.tile([P, CHUNK_COLS], BF16, name="adj_sb", tag="adj_sb")
-            nc.sync.dma_start(out=adj_sb[g][:], in_=chunk_rows(adj, g).rearrange("(p t) k -> p (t k)", t=4))
-            x0_sb[g] = inputs.tile([P, CHUNK_COLS], BF16, name="x0_sb", tag="x0_sb")
-            nc.sync.dma_start(out=x0_sb[g][:], in_=chunk_rows(x_0, g).rearrange("(p t) k -> p (t k)", t=4))
-
-        def store_unit(u):
-            rows = chunk_rows(out, u // 2).rearrange("(p t) c -> p t c", t=4)
-            first = 2 * (u % 2)
-            cols = slice((u % 2) * UNIT_COLS, (u % 2 + 1) * UNIT_COLS)
+        def load_tiles(dram, tiles, name, g, first, n):
+            if first == 0:
+                tiles[g] = inputs.tile([P, CHUNK_COLS], BF16, name=name, tag=name)
+            cols = slice(first * TILE_COLS, (first + n) * TILE_COLS)
             nc.sync.dma_start(
-                out=rows[:, first:first + 2, :], in_=s_sb[u // 2][:, cols].rearrange("p (t c) -> p t c", t=2)
+                out=tiles[g][:, cols].rearrange("p (t k) -> p t k", t=n), in_=chunk_rows(dram, g)[:, first:first + n, :]
             )
 
+        def load_chunk(g):
+            load_tiles(adj, adj_sb, "adj_sb", g, 0, 4)
+            load_tiles(x_0, x0_sb, "x0_sb", g, 0, 4)
+
+        def store_tiles(u, i, n):
+            first = 2 * (u % 2) + i
+            cols = slice(first * TILE_COLS, (first + n) * TILE_COLS)
+            nc.sync.dma_start(
+                out=chunk_rows(out, u // 2)[:, first:first + n, :],
+                in_=s_sb[u // 2][:, cols].rearrange("p (t c) -> p t c", t=n),
+            )
+
+        def store_unit(u):
+            if u < N_UNITS - 1:
+                store_tiles(u, 0, 2)
+            else:
+                store_tiles(u, 0, 1)
+                store_tiles(u, 1, 1)
+
         def quantise(pool, grouped, label):
-            codes = pool.tile([P, CHUNK_COLS // 4], U32, name="codes_" + label, tag="codes_" + label, align_bytes=64)
-            scales = pool.tile([P, CHUNK_COLS // 4], U8, name="scales_" + label, tag="scales_" + label, align_bytes=64)
+            n = grouped.shape[1] // 4
+            codes = pool.tile([P, n], U32, name="codes_" + label, tag="codes_" + label, align_bytes=64)
+            scales = pool.tile([P, n], U8, name="scales_" + label, tag="scales_" + label, align_bytes=64)
             nc.vector.quantize_mx(out=codes[:].bitcast(FP8X4), scales=scales[:], in_=grouped[:])
             return codes, scales
 
-        def regroup_weight(engine_is_gpsimd, raw, label):
+        def weight_operand(raw, label):
             grouped = const.tile([P, CHUNK_COLS], BF16, name="grouped_" + label, tag="grouped_" + label, align_bytes=64)
-            dst = grouped[:].rearrange("p (c t) -> p c t", t=4)
-            src = raw[:].rearrange("p t c -> p c t")
-            if engine_is_gpsimd:
-                nc.gpsimd.tensor_scalar(out=dst, in0=src, scalar1=1.0, scalar2=0.0, op0=ALU.mult, op1=ALU.add)
-            else:
-                nc.vector.tensor_copy(out=dst, in_=src)
-            return grouped
+            nc.vector.tensor_copy(
+                out=grouped[:].rearrange("p (c t) -> p c t", t=4), in_=raw[:].rearrange("p t c -> p c t")
+            )
+            return quantise(const, grouped, label)
 
-        def scale_x0(u):
-            on_gpsimd = stream.tile([P, TILE_COLS], F32, name="x0_gpsimd", tag="x0_gpsimd", bufs=2)
+        def scale_x0_scalar(u):
+            tile = stream.tile([P, TILE_COLS], F32, name="x0_scalar", tag="x0_scalar", bufs=4)
+            nc.scalar.activation(out=tile[:], in_=x0_sb[u // 2][:, tile_cols(u, 1)], func=ACT.Copy, scale=C_X0)
+            x0_scaled[u, 1] = tile
+
+        def scale_x0_gpsimd(u):
+            tile = stream.tile([P, TILE_COLS], F32, name="x0_gpsimd", tag="x0_gpsimd")
             nc.gpsimd.tensor_scalar(
-                out=on_gpsimd[:], in0=x0_sb[u // 2][:, tile_cols(u, 0)],
+                out=tile[:], in0=x0_sb[u // 2][:, tile_cols(u, 0)],
                 scalar1=C_X0, scalar2=0.0, op0=ALU.mult, op1=ALU.add,
             )
-            on_scalar = stream.tile([P, TILE_COLS], F32, name="x0_scalar", tag="x0_scalar")
-            nc.scalar.activation(out=on_scalar[:], in_=x0_sb[u // 2][:, tile_cols(u, 1)], func=ACT.Copy, scale=C_X0)
-            x0_scaled[u] = (on_gpsimd, on_scalar)
+            x0_scaled[u, 0] = tile
 
         def transpose_adj(u):
             g, half = divmod(u, 2)
-            bank = bank_a.tile([P, 4 * P], F32, name="adj_t", tag="adj_t")
+            adj_bank[u] = bank_a.tile([P, 4 * P], F32, name="adj_t", tag="adj_t")
             words = adj_sb[g][:].bitcast(F32)
             for i in range(4):
                 first = half * 4 * P + i * P
-                nc.tensor.transpose(bank[:, i * P:(i + 1) * P], words[:, first:first + P], identity[:])
-            if half == 0:
-                adj_grouped[g] = stream.tile([P, CHUNK_COLS], BF16, name="adj_grouped", tag="adj_grouped", align_bytes=64)
-            grouped_words = adj_grouped[g][:].bitcast(F32)[:, half * 4 * P:(half + 1) * 4 * P]
+                nc.tensor.transpose(adj_bank[u][:, i * P:(i + 1) * P], words[:, first:first + P], identity[:])
+
+        def regroup_adj(u):
+            adj_grouped[u] = stream.tile([P, UNIT_COLS], BF16, name="adj_grouped", tag="adj_grouped", align_bytes=64)
             nc.scalar.copy(
-                out=grouped_words.rearrange("p (t r v) -> p t r v", t=2, v=2),
-                in_=bank[:].rearrange("p (t v r) -> p t r v", t=2, v=2),
+                out=adj_grouped[u][:].bitcast(F32).rearrange("p (t r v) -> p t r v", t=2, v=2),
+                in_=adj_bank[u][:].rearrange("p (t v r) -> p t r v", t=2, v=2),
             )
 
-        def mx_product(pool, label, codes, scales, u, i, moving):
-            rows = slice(((u % 2) * 2 + i) * P, ((u % 2) * 2 + i + 1) * P)
+        def mx_product(pool, label, operand, i, moving):
+            rows = slice(i * P, (i + 1) * P)
             bank = pool.tile([P, TILE_COLS], F32, name=label, tag=label)
             nc.tensor.matmul_mx(
                 out=bank[:],
-                lhsT=codes[:, rows].bitcast(FP8X4), lhsT_scale=scales[:, rows],
+                lhsT=operand[0][:, rows].bitcast(FP8X4), lhsT_scale=operand[1][:, rows],
                 rhs=weights[moving][0][:].bitcast(FP8X4), rhs_scale=weights[moving][1][:],
                 start=True, stop=True,
             )
             return bank
 
         def first_product(u):
+            for i in range(2):
+                h_bank[u, i] = mx_product(bank_h, "h", adj_mx[u], i, "x")
+
+        def first_sum(u):
             g = u // 2
-            banks = [mx_product(bank_h, "h", adj_codes[g], adj_scales[g], u, i, "x") for i in range(2)]
             if u % 2 == 0:
                 s_sb[g] = results.tile([P, CHUNK_COLS], F32, name="s_sb", tag="s_sb")
             for i in range(2):
                 nc.vector.scalar_tensor_tensor(
-                    out=s_sb[g][:, tile_cols(u, i)], in0=banks[i][:], scalar=C_H, in1=x0_scaled[u][i][:],
+                    out=s_sb[g][:, tile_cols(u, i)], in0=h_bank[u, i][:], scalar=C_H, in1=x0_scaled[u, i][:],
                     op0=ALU.mult, op1=ALU.add,
                 )
 
         def transpose_s(u):
             g = u // 2
-            banks = []
             for i in range(2):
                 bank = bank_t.tile([P, 4 * P], F32, name="s_t", tag="s_t")
-                first = first_col(u, i)
+                first = tile_cols(u, i).start
                 for t in range(4):
                     nc.tensor.transpose(
                         bank[:, t * P:(t + 1) * P], s_sb[g][:, first + t * P:first + (t + 1) * P], identity[:]
                     )
-                banks.append(bank)
-            if u % 2 == 0:
-                m_grouped[g] = stream.tile([P, CHUNK_COLS], BF16, name="m_grouped", tag="m_grouped", align_bytes=64)
+                s_bank[u, i] = bank
+
+        def regroup_m(u):
+            m_grouped[u] = stream.tile([P, UNIT_COLS], BF16, name="m_grouped", tag="m_grouped", align_bytes=64)
             for i in range(2):
                 nc.scalar.activation(
-                    out=m_grouped[g][:, tile_cols(u, i)].rearrange("p (r t) -> p r t", t=4),
-                    in_=banks[i][:].rearrange("p (t r) -> p r t", t=4),
+                    out=m_grouped[u][:, i * TILE_COLS:(i + 1) * TILE_COLS].rearrange("p (r t) -> p r t", t=4),
+                    in_=s_bank[u, i][:].rearrange("p (t r) -> p r t", t=4),
                     func=ACT.Copy, scale=UNDO,
                 )
 
         def second_product(u):
-            g = u // 2
-            banks = [mx_product(bank_p, "p", m_codes[g], m_scales[g], u, i, "w") for i in range(2)]
             for i in range(2):
-                if u % 2 == 0 and i == 1:
-                    p_scaled[u] = stream.tile([P, TILE_COLS], F32, name="p_scaled", tag="p_scaled", bufs=2)
-                    nc.scalar.activation(out=p_scaled[u][:], in_=banks[i][:], func=ACT.Copy, scale=BETA)
-                else:
+                p_bank[u, i] = mx_product(bank_p, "p", m_mx[u], i, "w")
+
+        def by_gpsimd(u, i):
+            return u % 2 == 1 and i == 1 and u < N_UNITS - 3
+
+        def second_sum(u):
+            g = u // 2
+            for i in range(2):
+                if not by_gpsimd(u, i):
                     nc.vector.scalar_tensor_tensor(
-                        out=s_sb[g][:, tile_cols(u, i)], in0=banks[i][:], scalar=BETA, in1=s_sb[g][:, tile_cols(u, i)],
+                        out=s_sb[g][:, tile_cols(u, i)], in0=p_bank[u, i][:], scalar=BETA, in1=s_sb[g][:, tile_cols(u, i)],
                         op0=ALU.mult, op1=ALU.add,
                     )
-            if u % 2 == 1:
-                store_unit(u)
+
+        def scale_product(u):
+            if by_gpsimd(u, 1):
+                p_scaled[u] = stream.tile([P, TILE_COLS], F32, name="p_scaled", tag="p_scaled")
+                nc.scalar.activation(out=p_scaled[u][:], in_=p_bank[u, 1][:], func=ACT.Copy, scale=BETA)
 
         def finish_on_gpsimd(u):
-            cols = tile_cols(u, 1)
-            nc.gpsimd.tensor_tensor(out=s_sb[u // 2][:, cols], in0=p_scaled[u][:], in1=s_sb[u // 2][:, cols], op=ALU.add)
-            store_unit(u)
-
-        def live(u):
-            return 0 <= u < N_UNITS
+            if by_gpsimd(u, 1):
+                cols = tile_cols(u, 1)
+                nc.gpsimd.tensor_tensor(
+                    out=s_sb[u // 2][:, cols], in0=p_scaled[u][:], in1=s_sb[u // 2][:, cols], op=ALU.add
+                )
 
         identity = const.tile([P, P], F32, name="identity", tag="identity")
         make_identity(nc, identity[:])
 
-        adj_sb[0] = inputs.tile([P, CHUNK_COLS], BF16, name="adj_sb", tag="adj_sb")
-        nc.sync.dma_start(out=adj_sb[0][:], in_=chunk_rows(adj, 0).rearrange("(p t) k -> p (t k)", t=4))
         x_raw = const.tile([P, 4, FEATS], BF16, name="x_raw", tag="x_raw")
         nc.sync.dma_start(
             out=x_raw[:].rearrange("p (u e) c -> p u e c", u=2), in_=x.rearrange("(u p e) c -> p u e c", u=2, e=2)
         )
-        x0_sb[0] = inputs.tile([P, CHUNK_COLS], BF16, name="x0_sb", tag="x0_sb")
-        nc.sync.dma_start(out=x0_sb[0][:], in_=chunk_rows(x_0, 0).rearrange("(p t) k -> p (t k)", t=4))
+        for first in (0, 2):
+            load_tiles(adj, adj_sb, "adj_sb", 0, first, 2)
+            load_tiles(x_0, x0_sb, "x0_sb", 0, first, 2)
+        load_tiles(adj, adj_sb, "adj_sb", 1, 0, 4)
         w_raw = const.tile([P, 4, FEATS], BF16, name="w_raw", tag="w_raw")
         nc.sync.dma_start(out=w_raw[:], in_=weight1.rearrange("(t p) c -> p t c", p=P))
-        for g in range(1, LOADS_AHEAD):
+        load_tiles(x_0, x0_sb, "x0_sb", 1, 0, 4)
+        for g in range(2, LOADS_AHEAD):
             load_chunk(g)
 
-        weights["x"] = quantise(const, regroup_weight(False, x_raw, "x"), "x")
+        weights["x"] = weight_operand(x_raw, "x")
 
-        for j in range(-A_LEAD, N_UNITS + ADD_LAG - 1):
-            if j % 2 == 0:
-                g_m, g_adj = j // 2 - 2, j // 2 + 1
-                if 0 <= g_m < N_CHUNKS:
-                    m_codes[g_m], m_scales[g_m] = quantise(stream, m_grouped[g_m], "m")
-                if 0 <= g_adj < N_CHUNKS:
-                    adj_codes[g_adj], adj_scales[g_adj] = quantise(stream, adj_grouped[g_adj], "adj")
+        def live(u):
+            return 0 <= u < N_UNITS
+
+        for j in range(-2, N_UNITS + 6):
             if live(j):
                 first_product(j)
-            if live(j + X0_LEAD):
-                scale_x0(j + X0_LEAD)
-            if j == -1:
-                w_grouped = regroup_weight(True, w_raw, "w")
-            if j == 1:
-                weights["w"] = quantise(const, w_grouped, "w")
-            if j % 2 == 0 and live(j - ADD_LAG):
-                finish_on_gpsimd(j - ADD_LAG)
-            if live(j - P_LAG):
-                second_product(j - P_LAG)
-            if live(j - T_LAG):
-                transpose_s(j - T_LAG)
-            if live(j + A_LEAD):
-                transpose_adj(j + A_LEAD)
-            if j >= 0 and j % 2 == 0 and j // 2 + LOADS_AHEAD < N_CHUNKS:
-                load_chunk(j // 2 + LOADS_AHEAD)
+            if live(j - 2):
+                second_product(j - 2)
+            if live(j):
+                first_sum(j)
+            if live(j + 2):
+                scale_x0_scalar(j + 2)
+            if live(j + 1):
+                regroup_adj(j + 1)
+            if live(j - 1):
+                regroup_m(j - 1)
+            if live(j + 1):
+                scale_x0_gpsimd(j + 1)
+                adj_mx[j + 1] = quantise(stream, adj_grouped[j + 1], "adj")
+            if live(j + 2):
+                transpose_adj(j + 2)
+            if live(j):
+                transpose_s(j)
+            if live(j - 3):
+                scale_product(j - 3)
+            if live(j - 1):
+                if j == 1:
+                    weights["w"] = weight_operand(w_raw, "w")
+                m_mx[j - 1] = quantise(stream, m_grouped[j - 1], "m")
+            if live(j - 2):
+                second_sum(j - 2)
+            if live(j - 5):
+                finish_on_gpsimd(j - 5)
+            if live(j - 6):
+                store_unit(j - 6)
+            if j >= 2 and j % 2 == 0 and (j - 2) // 2 + LOADS_AHEAD < N_CHUNKS:
+                load_chunk((j - 2) // 2 + LOADS_AHEAD)

@@ -204,12 +204,13 @@ def tile_gcnlayer_pa_t_kernel(tc, x, x_0, adj, weight1, out):
         nc.sync.dma_start(
             out=x_raw[:].rearrange("p (u e) c -> p u e c", u=2), in_=x.rearrange("(u p e) c -> p u e c", u=2, e=2)
         )
-        for first in (0, 2):
-            load_tiles(adj, adj_sb, "adj_sb", 0, first, 2)
-            load_tiles(x_0, x0_sb, "x0_sb", 0, first, 2)
-        load_tiles(adj, adj_sb, "adj_sb", 1, 0, 4)
+        load_tiles(adj, adj_sb, "adj_sb", 0, 0, 2)
+        load_tiles(x_0, x0_sb, "x0_sb", 0, 0, 2)
+        load_tiles(adj, adj_sb, "adj_sb", 0, 2, 2)
         w_raw = const.tile([P, 4, FEATS], BF16, name="w_raw", tag="w_raw")
         nc.sync.dma_start(out=w_raw[:], in_=weight1.rearrange("(t p) c -> p t c", p=P))
+        load_tiles(x_0, x0_sb, "x0_sb", 0, 2, 2)
+        load_tiles(adj, adj_sb, "adj_sb", 1, 0, 4)
         load_tiles(x_0, x0_sb, "x0_sb", 1, 0, 4)
         for g in range(2, LOADS_AHEAD):
             load_chunk(g)
@@ -219,37 +220,38 @@ def tile_gcnlayer_pa_t_kernel(tc, x, x_0, adj, weight1, out):
         def live(u):
             return 0 <= u < N_UNITS
 
-        for j in range(-2, N_UNITS + 6):
+        for j in range(-3, N_UNITS + 7):
             if live(j):
                 first_product(j)
-            if live(j - 2):
-                second_product(j - 2)
+            if live(j - 4):
+                second_product(j - 4)
+            if live(j - 3):
+                m_mx[j - 3] = quantise(stream, m_grouped[j - 3], "m")
+            if live(j + 1):
+                adj_mx[j + 1] = quantise(stream, adj_grouped[j + 1], "adj")
+            if j == -1:
+                weights["w"] = weight_operand(w_raw, "w")
             if live(j):
                 first_sum(j)
-            if live(j + 2):
-                scale_x0_scalar(j + 2)
-            if live(j + 1):
-                regroup_adj(j + 1)
+            if live(j - 4):
+                second_sum(j - 4)
+            if live(j - 1):
+                transpose_s(j - 1)
+            if live(j + 3):
+                transpose_adj(j + 3)
             if live(j - 1):
                 regroup_m(j - 1)
+            if live(j + 3):
+                regroup_adj(j + 3)
+            if live(j + 2):
+                scale_x0_scalar(j + 2)
+            if live(j - 4):
+                scale_product(j - 4)
             if live(j + 1):
                 scale_x0_gpsimd(j + 1)
-                adj_mx[j + 1] = quantise(stream, adj_grouped[j + 1], "adj")
-            if live(j + 2):
-                transpose_adj(j + 2)
-            if live(j):
-                transpose_s(j)
-            if live(j - 3):
-                scale_product(j - 3)
-            if live(j - 1):
-                if j == 1:
-                    weights["w"] = weight_operand(w_raw, "w")
-                m_mx[j - 1] = quantise(stream, m_grouped[j - 1], "m")
-            if live(j - 2):
-                second_sum(j - 2)
-            if live(j - 5):
-                finish_on_gpsimd(j - 5)
             if live(j - 6):
-                store_unit(j - 6)
-            if j >= 2 and j % 2 == 0 and (j - 2) // 2 + LOADS_AHEAD < N_CHUNKS:
-                load_chunk((j - 2) // 2 + LOADS_AHEAD)
+                finish_on_gpsimd(j - 6)
+            if live(j - 7):
+                store_unit(j - 7)
+            if j >= 1 and j % 2 == 1 and (j - 1) // 2 + LOADS_AHEAD < N_CHUNKS:
+                load_chunk((j - 1) // 2 + LOADS_AHEAD)

@@ -43,10 +43,12 @@ def tile_gcnlayer_pa_t_kernel(tc, x, x_0, adj, weight1, out):
         ctx.enter_context(tc.manual_schedule())
 
         adj_sb, x0_sb, x0_scaled, s_sb, p_scaled = {}, {}, {}, {}, {}
-        adj_bank, adj_grouped, adj_mx = {}, {}, {}
-        s_bank, m_grouped, m_mx = {}, {}, {}
-        h_bank, p_bank = {}, {}
+        adj_bank, s_bank, h_bank, p_bank = {}, {}, {}, {}
+        grouped, operand = {}, {}
         weights = {}
+
+        def live(u):
+            return 0 <= u < N_UNITS
 
         def tile_cols(u, i):
             first = (u % 2) * UNIT_COLS + i * TILE_COLS
@@ -82,19 +84,26 @@ def tile_gcnlayer_pa_t_kernel(tc, x, x_0, adj, weight1, out):
                 store_tiles(u, 0, 1)
                 store_tiles(u, 1, 1)
 
-        def quantise(pool, grouped, label):
-            n = grouped.shape[1] // 4
-            codes = pool.tile([P, n], U32, name="codes_" + label, tag="codes_" + label, align_bytes=64)
-            scales = pool.tile([P, n], U8, name="scales_" + label, tag="scales_" + label, align_bytes=64)
-            nc.vector.quantize_mx(out=codes[:].bitcast(FP8X4), scales=scales[:], in_=grouped[:])
+        def quantise(pool, source, first, last, label):
+            codes = pool.tile([P, CHUNK_COLS // 4], U32, name="codes_" + label, tag="codes_" + label, align_bytes=64)
+            scales = pool.tile([P, CHUNK_COLS // 4], U8, name="scales_" + label, tag="scales_" + label, align_bytes=64)
+            words = slice(first // 4, last // 4)
+            nc.vector.quantize_mx(
+                out=codes[:, words].bitcast(FP8X4), scales=scales[:, words], in_=source[:, first:last]
+            )
             return codes, scales
 
+        def quantise_step(j):
+            first = 0 if live(j + 1) else UNIT_COLS
+            last = CHUNK_COLS if live(j - 3) else UNIT_COLS
+            operand[j] = quantise(stream, grouped[j], first, last, "step")
+
         def weight_operand(raw, label):
-            grouped = const.tile([P, CHUNK_COLS], BF16, name="grouped_" + label, tag="grouped_" + label, align_bytes=64)
+            regrouped = const.tile([P, CHUNK_COLS], BF16, name="grouped_" + label, tag="grouped_" + label, align_bytes=64)
             nc.vector.tensor_copy(
-                out=grouped[:].rearrange("p (c t) -> p c t", t=4), in_=raw[:].rearrange("p t c -> p c t")
+                out=regrouped[:].rearrange("p (c t) -> p c t", t=4), in_=raw[:].rearrange("p t c -> p c t")
             )
-            return quantise(const, grouped, label)
+            return quantise(const, regrouped, 0, CHUNK_COLS, label)
 
         def scale_x0_scalar(u):
             tile = stream.tile([P, TILE_COLS], F32, name="x0_scalar", tag="x0_scalar", bufs=4)
@@ -111,25 +120,28 @@ def tile_gcnlayer_pa_t_kernel(tc, x, x_0, adj, weight1, out):
 
         def transpose_adj(u):
             g, half = divmod(u, 2)
-            adj_bank[u] = bank_a.tile([P, 4 * P], F32, name="adj_t", tag="adj_t")
+            if u in (1, 2):
+                adj_bank[u] = bank_p.tile([P, 4 * P], F32, name="adj_t_head", tag="p")
+            else:
+                adj_bank[u] = bank_a.tile([P, 4 * P], F32, name="adj_t", tag="adj_t")
             words = adj_sb[g][:].bitcast(F32)
             for i in range(4):
                 first = half * 4 * P + i * P
                 nc.tensor.transpose(adj_bank[u][:, i * P:(i + 1) * P], words[:, first:first + P], identity[:])
 
         def regroup_adj(u):
-            adj_grouped[u] = stream.tile([P, UNIT_COLS], BF16, name="adj_grouped", tag="adj_grouped", align_bytes=64)
             nc.scalar.copy(
-                out=adj_grouped[u][:].bitcast(F32).rearrange("p (t r v) -> p t r v", t=2, v=2),
+                out=grouped[u - 1][:, :UNIT_COLS].bitcast(F32).rearrange("p (t r v) -> p t r v", t=2, v=2),
                 in_=adj_bank[u][:].rearrange("p (t v r) -> p t r v", t=2, v=2),
             )
 
-        def mx_product(pool, label, operand, i, moving):
-            rows = slice(i * P, (i + 1) * P)
+        def mx_product(pool, label, step, tile, moving):
+            codes, scales = operand[step]
+            rows = slice(tile * P, (tile + 1) * P)
             bank = pool.tile([P, TILE_COLS], F32, name=label, tag=label)
             nc.tensor.matmul_mx(
                 out=bank[:],
-                lhsT=operand[0][:, rows].bitcast(FP8X4), lhsT_scale=operand[1][:, rows],
+                lhsT=codes[:, rows].bitcast(FP8X4), lhsT_scale=scales[:, rows],
                 rhs=weights[moving][0][:].bitcast(FP8X4), rhs_scale=weights[moving][1][:],
                 start=True, stop=True,
             )
@@ -137,7 +149,7 @@ def tile_gcnlayer_pa_t_kernel(tc, x, x_0, adj, weight1, out):
 
         def first_product(u):
             for i in range(2):
-                h_bank[u, i] = mx_product(bank_h, "h", adj_mx[u], i, "x")
+                h_bank[u, i] = mx_product(bank_h, "h", u - 1, i, "x")
 
         def first_sum(u):
             g = u // 2
@@ -161,17 +173,17 @@ def tile_gcnlayer_pa_t_kernel(tc, x, x_0, adj, weight1, out):
                 s_bank[u, i] = bank
 
         def regroup_m(u):
-            m_grouped[u] = stream.tile([P, UNIT_COLS], BF16, name="m_grouped", tag="m_grouped", align_bytes=64)
             for i in range(2):
+                first = UNIT_COLS + i * TILE_COLS
                 nc.scalar.activation(
-                    out=m_grouped[u][:, i * TILE_COLS:(i + 1) * TILE_COLS].rearrange("p (r t) -> p r t", t=4),
+                    out=grouped[u + 3][:, first:first + TILE_COLS].rearrange("p (r t) -> p r t", t=4),
                     in_=s_bank[u, i][:].rearrange("p (t r) -> p r t", t=4),
                     func=ACT.Copy, scale=UNDO,
                 )
 
         def second_product(u):
             for i in range(2):
-                p_bank[u, i] = mx_product(bank_p, "p", m_mx[u], i, "w")
+                p_bank[u, i] = mx_product(bank_p, "p", u + 3, 2 + i, "w")
 
         def by_gpsimd(u, i):
             return u % 2 == 1 and i == 1 and u < N_UNITS - 3
@@ -205,32 +217,37 @@ def tile_gcnlayer_pa_t_kernel(tc, x, x_0, adj, weight1, out):
             out=x_raw[:].rearrange("p (u e) c -> p u e c", u=2), in_=x.rearrange("(u p e) c -> p u e c", u=2, e=2)
         )
         load_tiles(adj, adj_sb, "adj_sb", 0, 0, 2)
-        load_tiles(x_0, x0_sb, "x0_sb", 0, 0, 2)
         load_tiles(adj, adj_sb, "adj_sb", 0, 2, 2)
+        load_tiles(x_0, x0_sb, "x0_sb", 0, 0, 2)
+        load_tiles(adj, adj_sb, "adj_sb", 1, 0, 2)
+        load_tiles(x_0, x0_sb, "x0_sb", 0, 2, 2)
         w_raw = const.tile([P, 4, FEATS], BF16, name="w_raw", tag="w_raw")
         nc.sync.dma_start(out=w_raw[:], in_=weight1.rearrange("(t p) c -> p t c", p=P))
-        load_tiles(x_0, x0_sb, "x0_sb", 0, 2, 2)
-        load_tiles(adj, adj_sb, "adj_sb", 1, 0, 4)
+        load_tiles(adj, adj_sb, "adj_sb", 1, 2, 2)
         load_tiles(x_0, x0_sb, "x0_sb", 1, 0, 4)
         for g in range(2, LOADS_AHEAD):
             load_chunk(g)
 
         weights["x"] = weight_operand(x_raw, "x")
 
-        def live(u):
-            return 0 <= u < N_UNITS
+        w_grouped = const.tile([P, CHUNK_COLS], BF16, name="w_grouped", tag="w_grouped", align_bytes=64)
+
+        def regroup_weight_part(q):
+            cols = slice(q * P, (q + 1) * P)
+            nc.gpsimd.tensor_scalar(
+                out=w_grouped[:].rearrange("p (c t) -> p c t", t=4)[:, cols, :], in0=w_raw[:].rearrange("p t c -> p c t")[:, cols, :],
+                scalar1=1.0, scalar2=0.0, op0=ALU.mult, op1=ALU.add,
+            )
 
         for j in range(-3, N_UNITS + 7):
             if live(j):
                 first_product(j)
             if live(j - 4):
                 second_product(j - 4)
-            if live(j - 3):
-                m_mx[j - 3] = quantise(stream, m_grouped[j - 3], "m")
-            if live(j + 1):
-                adj_mx[j + 1] = quantise(stream, adj_grouped[j + 1], "adj")
-            if j == -1:
-                weights["w"] = weight_operand(w_raw, "w")
+            if live(j + 1) or live(j - 3):
+                quantise_step(j)
+            if j == 3:
+                weights["w"] = quantise(const, w_grouped, 0, CHUNK_COLS, "w")
             if live(j):
                 first_sum(j)
             if live(j - 4):
@@ -239,6 +256,8 @@ def tile_gcnlayer_pa_t_kernel(tc, x, x_0, adj, weight1, out):
                 transpose_s(j - 1)
             if live(j + 3):
                 transpose_adj(j + 3)
+            if live(j + 3) or live(j - 1):
+                grouped[j + 2] = stream.tile([P, CHUNK_COLS], BF16, name="grouped", tag="grouped", align_bytes=64)
             if live(j - 1):
                 regroup_m(j - 1)
             if live(j + 3):
@@ -249,6 +268,8 @@ def tile_gcnlayer_pa_t_kernel(tc, x, x_0, adj, weight1, out):
                 scale_product(j - 4)
             if live(j + 1):
                 scale_x0_gpsimd(j + 1)
+            if -1 <= j < 3:
+                regroup_weight_part(j + 1)
             if live(j - 6):
                 finish_on_gpsimd(j - 6)
             if live(j - 7):

@@ -111,7 +111,7 @@ def tile_gcnlayer_pa_t_kernel(tc, x, x_0, adj, weight1, out):
             x0_scaled[u, 1] = tile
 
         def scale_x0_gpsimd(u):
-            tile = stream.tile([P, TILE_COLS], F32, name="x0_gpsimd", tag="x0_gpsimd")
+            tile = stream.tile([P, TILE_COLS], F32, name="x0_gpsimd", tag="x0_gpsimd", bufs=2)
             nc.gpsimd.tensor_scalar(
                 out=tile[:], in0=x0_sb[u // 2][:, tile_cols(u, 0)],
                 scalar1=C_X0, scalar2=0.0, op0=ALU.mult, op1=ALU.add,
@@ -252,27 +252,27 @@ def tile_gcnlayer_pa_t_kernel(tc, x, x_0, adj, weight1, out):
                 first_sum(j)
             if live(j - 4):
                 second_sum(j - 4)
-            if live(j - 1):
-                transpose_s(j - 1)
             if live(j + 3):
                 transpose_adj(j + 3)
+            if live(j - 1):
+                transpose_s(j - 1)
             if live(j + 3) or live(j - 1):
                 grouped[j + 2] = stream.tile([P, CHUNK_COLS], BF16, name="grouped", tag="grouped", align_bytes=64)
+            if live(j - 4):
+                scale_product(j - 4)
+            if live(j + 3):
+                regroup_adj(j + 3)
             if live(j - 1):
                 regroup_m(j - 1)
             if live(j + 3):
-                regroup_adj(j + 3)
-            if live(j + 2):
-                scale_x0_scalar(j + 2)
-            if live(j - 4):
-                scale_product(j - 4)
+                scale_x0_scalar(j + 3)
+            if live(j - 5):
+                finish_on_gpsimd(j - 5)
             if live(j + 1):
                 scale_x0_gpsimd(j + 1)
             if -1 <= j < 3:
                 regroup_weight_part(j + 1)
             if live(j - 6):
-                finish_on_gpsimd(j - 6)
-            if live(j - 7):
-                store_unit(j - 7)
+                store_unit(j - 6)
             if j >= 1 and j % 2 == 1 and (j - 1) // 2 + LOADS_AHEAD < N_CHUNKS:
                 load_chunk((j - 1) // 2 + LOADS_AHEAD)

@@ -108,15 +108,17 @@ def tile_gcnlayer_pa_t_kernel(tc, x, x_0, adj, weight1, out):
         def scale_x0_scalar(u):
             tile = stream.tile([P, TILE_COLS], F32, name="x0_scalar", tag="x0_scalar", bufs=4)
             nc.scalar.activation(out=tile[:], in_=x0_sb[u // 2][:, tile_cols(u, 1)], func=ACT.Copy, scale=C_X0)
-            x0_scaled[u, 1] = tile
+            x0_scaled[u, 1] = tile[:]
 
-        def scale_x0_gpsimd(u):
-            tile = stream.tile([P, TILE_COLS], F32, name="x0_gpsimd", tag="x0_gpsimd", bufs=2)
+        def scale_x0_gpsimd(g):
+            tile = stream.tile([P, UNIT_COLS], F32, name="x0_gpsimd", tag="x0_gpsimd", bufs=2)
             nc.gpsimd.tensor_scalar(
-                out=tile[:], in0=x0_sb[u // 2][:, tile_cols(u, 0)],
+                out=tile[:].rearrange("p (u k) -> p u k", u=2),
+                in0=x0_sb[g][:].rearrange("p (u i k) -> p u i k", u=2, i=2)[:, :, 0, :],
                 scalar1=C_X0, scalar2=0.0, op0=ALU.mult, op1=ALU.add,
             )
-            x0_scaled[u, 0] = tile
+            for half in range(2):
+                x0_scaled[2 * g + half, 0] = tile[:, half * TILE_COLS:(half + 1) * TILE_COLS]
 
         def transpose_adj(u):
             g, half = divmod(u, 2)
@@ -157,7 +159,7 @@ def tile_gcnlayer_pa_t_kernel(tc, x, x_0, adj, weight1, out):
                 s_sb[g] = results.tile([P, CHUNK_COLS], F32, name="s_sb", tag="s_sb")
             for i in range(2):
                 nc.vector.scalar_tensor_tensor(
-                    out=s_sb[g][:, tile_cols(u, i)], in0=h_bank[u, i][:], scalar=C_H, in1=x0_scaled[u, i][:],
+                    out=s_sb[g][:, tile_cols(u, i)], in0=h_bank[u, i][:], scalar=C_H, in1=x0_scaled[u, i],
                     op0=ALU.mult, op1=ALU.add,
                 )
 
@@ -208,6 +210,11 @@ def tile_gcnlayer_pa_t_kernel(tc, x, x_0, adj, weight1, out):
                 nc.gpsimd.tensor_tensor(
                     out=s_sb[u // 2][:, cols], in0=p_scaled[u][:], in1=s_sb[u // 2][:, cols], op=ALU.add
                 )
+
+        def hold_gpsimd(u):
+            last = tile_cols(u, 0 if by_gpsimd(u, 1) else 1).stop - 1
+            probe = stream.tile([P, 1], F32, name="probe", tag="probe")
+            nc.gpsimd.tensor_copy(out=probe[:], in_=s_sb[u // 2][:, last:last + 1])
 
         identity = const.tile([P, P], F32, name="identity", tag="identity")
         make_identity(nc, identity[:])
@@ -267,9 +274,11 @@ def tile_gcnlayer_pa_t_kernel(tc, x, x_0, adj, weight1, out):
             if live(j + 3):
                 scale_x0_scalar(j + 3)
             if live(j - 5):
+                hold_gpsimd(j - 5)
+            if live(j - 5):
                 finish_on_gpsimd(j - 5)
-            if live(j + 1):
-                scale_x0_gpsimd(j + 1)
+            if j % 2 == 1 and live(j + 1):
+                scale_x0_gpsimd((j + 1) // 2)
             if -1 <= j < 3:
                 regroup_weight_part(j + 1)
             if live(j - 6):

@@ -26,7 +26,7 @@ CHUNK_COLS = 2 * UNIT_COLS
 CHUNK_ROWS = 4 * P
 N_CHUNKS = ROWS // CHUNK_ROWS
 N_UNITS = 2 * N_CHUNKS
-LOADS_AHEAD = 6
+LOADS_AHEAD = 4
 
 
 def tile_gcnlayer_pa_t_kernel(tc, x, x_0, adj, weight1, out):
@@ -35,7 +35,7 @@ def tile_gcnlayer_pa_t_kernel(tc, x, x_0, adj, weight1, out):
         const = ctx.enter_context(tc.tile_pool(name="const", bufs=1))
         inputs = ctx.enter_context(tc.tile_pool(name="inputs", bufs=LOADS_AHEAD))
         stream = ctx.enter_context(tc.tile_pool(name="stream", bufs=3))
-        results = ctx.enter_context(tc.tile_pool(name="results", bufs=7))
+        results = ctx.enter_context(tc.tile_pool(name="results", bufs=16))
         bank_a = ctx.enter_context(tc.psum_pool(name="bank_a", bufs=1))
         bank_h = ctx.enter_context(tc.psum_pool(name="bank_h", bufs=2))
         bank_t = ctx.enter_context(tc.psum_pool(name="bank_t", bufs=2))
@@ -137,10 +137,10 @@ def tile_gcnlayer_pa_t_kernel(tc, x, x_0, adj, weight1, out):
                 in_=adj_bank[u][:].rearrange("p (t v r) -> p t r v", t=2, v=2),
             )
 
-        def mx_product(pool, label, step, tile, moving):
+        def mx_product(pool, label, step, tile, moving, tag=None):
             codes, scales = operand[step]
             rows = slice(tile * P, (tile + 1) * P)
-            bank = pool.tile([P, TILE_COLS], F32, name=label, tag=label)
+            bank = pool.tile([P, TILE_COLS], F32, name=label, tag=tag or label)
             nc.tensor.matmul_mx(
                 out=bank[:],
                 lhsT=codes[:, rows].bitcast(FP8X4), lhsT_scale=scales[:, rows],
@@ -151,7 +151,10 @@ def tile_gcnlayer_pa_t_kernel(tc, x, x_0, adj, weight1, out):
 
         def first_product(u):
             for i in range(2):
-                h_bank[u, i] = mx_product(bank_h, "h", u - 1, i, "x")
+                if u in (1, 3):
+                    h_bank[u, i] = mx_product(bank_p, "h", u - 1, i, "x", "p")
+                else:
+                    h_bank[u, i] = mx_product(bank_h, "h", u - 1, i, "x")
 
         def first_sum(u):
             g = u // 2
@@ -188,7 +191,7 @@ def tile_gcnlayer_pa_t_kernel(tc, x, x_0, adj, weight1, out):
                 p_bank[u, i] = mx_product(bank_p, "p", u + 3, 2 + i, "w")
 
         def by_gpsimd(u, i):
-            return u % 2 == 1 and i == 1 and u < N_UNITS - 3
+            return u % 2 == 1 and i == 1 and u < N_UNITS - 5
 
         def second_sum(u):
             g = u // 2
@@ -225,17 +228,22 @@ def tile_gcnlayer_pa_t_kernel(tc, x, x_0, adj, weight1, out):
         )
         load_tiles(adj, adj_sb, "adj_sb", 0, 0, 2)
         load_tiles(adj, adj_sb, "adj_sb", 0, 2, 2)
-        load_tiles(x_0, x0_sb, "x0_sb", 0, 0, 2)
-        load_tiles(adj, adj_sb, "adj_sb", 1, 0, 2)
-        load_tiles(x_0, x0_sb, "x0_sb", 0, 2, 2)
+        load_tiles(x_0, x0_sb, "x0_sb", 0, 0, 4)
+        load_tiles(adj, adj_sb, "adj_sb", 1, 0, 4)
+        load_tiles(x_0, x0_sb, "x0_sb", 1, 0, 4)
+        load_tiles(adj, adj_sb, "adj_sb", 2, 0, 2)
         w_raw = const.tile([P, 4, FEATS], BF16, name="w_raw", tag="w_raw")
         nc.sync.dma_start(out=w_raw[:], in_=weight1.rearrange("(t p) c -> p t c", p=P))
-        load_tiles(adj, adj_sb, "adj_sb", 1, 2, 2)
-        load_tiles(x_0, x0_sb, "x0_sb", 1, 0, 4)
-        for g in range(2, LOADS_AHEAD):
+        load_tiles(adj, adj_sb, "adj_sb", 2, 2, 2)
+        load_tiles(x_0, x0_sb, "x0_sb", 2, 0, 4)
+        for g in range(3, LOADS_AHEAD):
             load_chunk(g)
 
-        weights["x"] = weight_operand(x_raw, "x")
+        x_grouped = const.tile([P, CHUNK_COLS], BF16, name="x_grouped", tag="x_grouped", align_bytes=64)
+        x_dst, x_src = x_grouped[:].rearrange("p (c t) -> p c t", t=4), x_raw[:].rearrange("p t c -> p c t")
+        nc.vector.tensor_copy(out=x_dst[:, :320, :], in_=x_src[:, :320, :])
+        nc.scalar.copy(out=x_dst[:, 320:, :], in_=x_src[:, 320:, :])
+        weights["x"] = quantise(const, x_grouped, 0, CHUNK_COLS, "x")
 
         w_grouped = const.tile([P, CHUNK_COLS], BF16, name="w_grouped", tag="w_grouped", align_bytes=64)
 
@@ -279,8 +287,9 @@ def tile_gcnlayer_pa_t_kernel(tc, x, x_0, adj, weight1, out):
                 finish_on_gpsimd(j - 5)
             if j % 2 == 1 and live(j + 1):
                 scale_x0_gpsimd((j + 1) // 2)
-            if -1 <= j < 3:
-                regroup_weight_part(j + 1)
+            if 1 <= j < 3:
+                regroup_weight_part(2 * j - 2)
+                regroup_weight_part(2 * j - 1)
             if live(j - 6):
                 store_unit(j - 6)
             if j >= 1 and j % 2 == 1 and (j - 1) // 2 + LOADS_AHEAD < N_CHUNKS:

@@ -161,10 +161,17 @@ def tile_gcnlayer_pa_t_kernel(tc, x, x_0, adj, weight1, out):
             if u % 2 == 0:
                 s_sb[g] = results.tile([P, CHUNK_COLS], F32, name="s_sb", tag="s_sb")
             for i in range(2):
-                nc.vector.scalar_tensor_tensor(
-                    out=s_sb[g][:, tile_cols(u, i)], in0=h_bank[u, i][:], scalar=C_H, in1=x0_scaled[u, i],
-                    op0=ALU.mult, op1=ALU.add,
-                )
+                cols = tile_cols(u, i)
+                if by_gpsimd(u, i):
+                    nc.vector.scalar_tensor_tensor(
+                        out=s_sb[g][:, cols], in0=x0_sb[g][:, cols], scalar=C_X0 / C_H, in1=h_bank[u, i][:],
+                        op0=ALU.mult, op1=ALU.add,
+                    )
+                else:
+                    nc.vector.scalar_tensor_tensor(
+                        out=s_sb[g][:, cols], in0=h_bank[u, i][:], scalar=C_H, in1=x0_scaled[u, i],
+                        op0=ALU.mult, op1=ALU.add,
+                    )
 
         def transpose_s(u):
             g = u // 2
@@ -183,12 +190,15 @@ def tile_gcnlayer_pa_t_kernel(tc, x, x_0, adj, weight1, out):
                 nc.scalar.activation(
                     out=grouped[u + 3][:, first:first + TILE_COLS].rearrange("p (r t) -> p r t", t=4),
                     in_=s_bank[u, i][:].rearrange("p (t r) -> p r t", t=4),
-                    func=ACT.Copy, scale=UNDO,
+                    func=ACT.Copy, scale=0.9 if by_gpsimd(u, i) else UNDO,
                 )
 
         def second_product(u):
             for i in range(2):
-                p_bank[u, i] = mx_product(bank_p, "p", u + 3, 2 + i, "w")
+                if u >= 28 and i == 1:
+                    p_bank[u, i] = mx_product(bank_h, "p", u + 3, 2 + i, "w", "h")
+                else:
+                    p_bank[u, i] = mx_product(bank_p, "p", u + 3, 2 + i, "w")
 
         def by_gpsimd(u, i):
             return u % 2 == 1 and i == 1 and u < N_UNITS - 5
@@ -212,6 +222,13 @@ def tile_gcnlayer_pa_t_kernel(tc, x, x_0, adj, weight1, out):
                 cols = tile_cols(u, 1)
                 nc.gpsimd.tensor_tensor(
                     out=s_sb[u // 2][:, cols], in0=p_scaled[u][:], in1=s_sb[u // 2][:, cols], op=ALU.add
+                )
+
+        def scale_sum(u):
+            if by_gpsimd(u, 1):
+                cols = tile_cols(u, 1)
+                nc.gpsimd.tensor_scalar(
+                    out=s_sb[u // 2][:, cols], in0=s_sb[u // 2][:, cols], scalar1=C_H, scalar2=0.0, op0=ALU.mult, op1=ALU.add
                 )
 
         def hold_gpsimd(u):
@@ -279,7 +296,7 @@ def tile_gcnlayer_pa_t_kernel(tc, x, x_0, adj, weight1, out):
                 regroup_adj(j + 3)
             if live(j - 1):
                 regroup_m(j - 1)
-            if live(j + 3):
+            if live(j + 3) and not by_gpsimd(j + 3, 1):
                 scale_x0_scalar(j + 3)
             if live(j - 5):
                 hold_gpsimd(j - 5)
@@ -287,6 +304,8 @@ def tile_gcnlayer_pa_t_kernel(tc, x, x_0, adj, weight1, out):
                 finish_on_gpsimd(j - 5)
             if j % 2 == 1 and live(j + 1):
                 scale_x0_gpsimd((j + 1) // 2)
+            if live(j - 4):
+                scale_sum(j - 4)
             if 1 <= j < 3:
                 regroup_weight_part(2 * j - 2)
                 regroup_weight_part(2 * j - 1)

from contextlib import ExitStack

import concourse.mybir as mybir
from concourse.masks import make_identity

F32 = mybir.dt.float32
BF16 = mybir.dt.bfloat16
U32 = mybir.dt.uint32
U8 = mybir.dt.uint8
FP8X4 = mybir.dt.float8_e4m3fn_x4
ALU = mybir.AluOpType
ACT = mybir.ActivationFunctionType

P = 128
ROWS, NODES, FEATS = 8192, 512, 512
FLOPS = 2 * ROWS * NODES * FEATS + 2 * ROWS * FEATS * FEATS

BETA = 0.11778303565638346
C_H = (1.0 - BETA) * 0.9
C_X0 = (1.0 - BETA) * 0.1
UNDO = 1.0 / (1.0 - BETA)

TILE_COLS = 512
UNIT_COLS = 2 * TILE_COLS
CHUNK_COLS = 2 * UNIT_COLS
CHUNK_ROWS = 4 * P
N_CHUNKS = ROWS // CHUNK_ROWS
N_UNITS = 2 * N_CHUNKS
LOADS_AHEAD = 4


def tile_gcnlayer_pa_t_kernel(tc, x, x_0, adj, weight1, out):
    nc = tc.nc
    with ExitStack() as ctx:
        const = ctx.enter_context(tc.tile_pool(name="const", bufs=1))
        inputs = ctx.enter_context(tc.tile_pool(name="inputs", bufs=LOADS_AHEAD))
        stream = ctx.enter_context(tc.tile_pool(name="stream", bufs=3))
        results = ctx.enter_context(tc.tile_pool(name="results", bufs=16))
        bank_a = ctx.enter_context(tc.psum_pool(name="bank_a", bufs=1))
        bank_h = ctx.enter_context(tc.psum_pool(name="bank_h", bufs=2))
        bank_t = ctx.enter_context(tc.psum_pool(name="bank_t", bufs=2))
        bank_p = ctx.enter_context(tc.psum_pool(name="bank_p", bufs=3))
        ctx.enter_context(tc.manual_schedule())

        adj_sb, x0_sb, x0_scaled, s_sb, p_scaled = {}, {}, {}, {}, {}
        adj_bank, s_bank, h_bank, p_bank = {}, {}, {}, {}
        grouped, operand = {}, {}
        weights = {}

        def live(u):
            return 0 <= u < N_UNITS

        def tile_cols(u, i):
            first = (u % 2) * UNIT_COLS + i * TILE_COLS
            return slice(first, first + TILE_COLS)

        def chunk_rows(dram, g):
            return dram[g * CHUNK_ROWS:(g + 1) * CHUNK_ROWS, :].rearrange("(p t) k -> p t k", t=4)

        def load_tiles(dram, tiles, name, g, first, n):
            if first == 0:
                tiles[g] = inputs.tile([P, CHUNK_COLS], BF16, name=name, tag=name)
            cols = slice(first * TILE_COLS, (first + n) * TILE_COLS)
            nc.sync.dma_start(
                out=tiles[g][:, cols].rearrange("p (t k) -> p t k", t=n), in_=chunk_rows(dram, g)[:, first:first + n, :]
            )

        def load_chunk(g):
            load_tiles(adj, adj_sb, "adj_sb", g, 0, 4)
            load_tiles(x_0, x0_sb, "x0_sb", g, 0, 4)

        def store_tiles(u, i, n):
            first = 2 * (u % 2) + i
            cols = slice(first * TILE_COLS, (first + n) * TILE_COLS)
            nc.sync.dma_start(
                out=chunk_rows(out, u // 2)[:, first:first + n, :],
                in_=s_sb[u // 2][:, cols].rearrange("p (t c) -> p t c", t=n),
            )

        def store_unit(u):
            if u < N_UNITS - 1:
                store_tiles(u, 0, 2)
            else:
                store_tiles(u, 0, 1)
                store_tiles(u, 1, 1)

        def quantise(pool, source, first, last, label):
            codes = pool.tile([P, CHUNK_COLS // 4], U32, name="codes_" + label, tag="codes_" + label, align_bytes=64)
            scales = pool.tile([P, CHUNK_COLS // 4], U8, name="scales_" + label, tag="scales_" + label, align_bytes=64)
            words = slice(first // 4, last // 4)
            nc.vector.quantize_mx(
                out=codes[:, words].bitcast(FP8X4), scales=scales[:, words], in_=source[:, first:last]
            )
            return codes, scales

        def quantise_step(j):
            first = 0 if live(j + 1) else UNIT_COLS
            last = CHUNK_COLS if live(j - 3) else UNIT_COLS
            operand[j] = quantise(stream, grouped[j], first, last, "step")

        def weight_operand(raw, label):
            regrouped = const.tile([P, CHUNK_COLS], BF16, name="grouped_" + label, tag="grouped_" + label, align_bytes=64)
            nc.vector.tensor_copy(
                out=regrouped[:].rearrange("p (c t) -> p c t", t=4), in_=raw[:].rearrange("p t c -> p c t")
            )
            return quantise(const, regrouped, 0, CHUNK_COLS, label)

        def scale_x0_scalar(u):
            tile = stream.tile([P, TILE_COLS], F32, name="x0_scalar", tag="x0_scalar", bufs=4)
            nc.scalar.activation(out=tile[:], in_=x0_sb[u // 2][:, tile_cols(u, 1)], func=ACT.Copy, scale=C_X0)
            x0_scaled[u, 1] = tile[:]

        def scale_x0_gpsimd(g):
            tile = stream.tile([P, UNIT_COLS], F32, name="x0_gpsimd", tag="x0_gpsimd", bufs=2)
            nc.gpsimd.tensor_scalar(
                out=tile[:].rearrange("p (u k) -> p u k", u=2),
                in0=x0_sb[g][:].rearrange("p (u i k) -> p u i k", u=2, i=2)[:, :, 0, :],
                scalar1=C_X0, scalar2=0.0, op0=ALU.mult, op1=ALU.add,
            )
            for half in range(2):
                x0_scaled[2 * g + half, 0] = tile[:, half * TILE_COLS:(half + 1) * TILE_COLS]

        def transpose_adj(u):
            g, half = divmod(u, 2)
            if u in (1, 2):
                adj_bank[u] = bank_p.tile([P, 4 * P], F32, name="adj_t_head", tag="p")
            else:
                adj_bank[u] = bank_a.tile([P, 4 * P], F32, name="adj_t", tag="adj_t")
            words = adj_sb[g][:].bitcast(F32)
            for i in range(4):
                first = half * 4 * P + i * P
                nc.tensor.transpose(adj_bank[u][:, i * P:(i + 1) * P], words[:, first:first + P], identity[:])

        def regroup_adj(u):
            nc.scalar.copy(
                out=grouped[u - 1][:, :UNIT_COLS].bitcast(F32).rearrange("p (t r v) -> p t r v", t=2, v=2),
                in_=adj_bank[u][:].rearrange("p (t v r) -> p t r v", t=2, v=2),
            )

        def mx_product(pool, label, step, tile, moving, tag=None):
            codes, scales = operand[step]
            rows = slice(tile * P, (tile + 1) * P)
            bank = pool.tile([P, TILE_COLS], F32, name=label, tag=tag or label)
            nc.tensor.matmul_mx(
                out=bank[:],
                lhsT=codes[:, rows].bitcast(FP8X4), lhsT_scale=scales[:, rows],
                rhs=weights[moving][0][:].bitcast(FP8X4), rhs_scale=weights[moving][1][:],
                start=True, stop=True,
            )
            return bank

        def first_product(u):
            for i in range(2):
                if u in (1, 3):
                    h_bank[u, i] = mx_product(bank_p, "h", u - 1, i, "x", "p")
                else:
                    h_bank[u, i] = mx_product(bank_h, "h", u - 1, i, "x")

        def first_sum(u):
            g = u // 2
            if u % 2 == 0:
                s_sb[g] = results.tile([P, CHUNK_COLS], F32, name="s_sb", tag="s_sb")
            for i in range(2):
                cols = tile_cols(u, i)
                if by_gpsimd(u, i):
                    nc.vector.scalar_tensor_tensor(
                        out=s_sb[g][:, cols], in0=x0_sb[g][:, cols], scalar=C_X0 / C_H, in1=h_bank[u, i][:],
                        op0=ALU.mult, op1=ALU.add,
                    )
                else:
                    nc.vector.scalar_tensor_tensor(
                        out=s_sb[g][:, cols], in0=h_bank[u, i][:], scalar=C_H, in1=x0_scaled[u, i],
                        op0=ALU.mult, op1=ALU.add,
                    )

        def transpose_s(u):
            g = u // 2
            for i in range(2):
                bank = bank_t.tile([P, 4 * P], F32, name="s_t", tag="s_t")
                first = tile_cols(u, i).start
                for t in range(4):
                    nc.tensor.transpose(
                        bank[:, t * P:(t + 1) * P], s_sb[g][:, first + t * P:first + (t + 1) * P], identity[:]
                    )
                s_bank[u, i] = bank

        def regroup_m(u):
            for i in range(2):
                first = UNIT_COLS + i * TILE_COLS
                nc.scalar.activation(
                    out=grouped[u + 3][:, first:first + TILE_COLS].rearrange("p (r t) -> p r t", t=4),
                    in_=s_bank[u, i][:].rearrange("p (t r) -> p r t", t=4),
                    func=ACT.Copy, scale=0.9 if by_gpsimd(u, i) else UNDO,
                )

        def second_product(u):
            for i in range(2):
                if u >= 28 and i == 1:
                    p_bank[u, i] = mx_product(bank_h, "p", u + 3, 2 + i, "w", "h")
                else:
                    p_bank[u, i] = mx_product(bank_p, "p", u + 3, 2 + i, "w")

        def by_gpsimd(u, i):
            return u % 2 == 1 and i == 1 and u < N_UNITS - 5

        def second_sum(u):
            g = u // 2
            for i in range(2):
                if not by_gpsimd(u, i):
                    nc.vector.scalar_tensor_tensor(
                        out=s_sb[g][:, tile_cols(u, i)], in0=p_bank[u, i][:], scalar=BETA, in1=s_sb[g][:, tile_cols(u, i)],
                        op0=ALU.mult, op1=ALU.add,
                    )

        def scale_product(u):
            if by_gpsimd(u, 1):
                p_scaled[u] = stream.tile([P, TILE_COLS], F32, name="p_scaled", tag="p_scaled")
                nc.scalar.activation(out=p_scaled[u][:], in_=p_bank[u, 1][:], func=ACT.Copy, scale=BETA)

        def finish_on_gpsimd(u):
            if by_gpsimd(u, 1):
                cols = tile_cols(u, 1)
                nc.gpsimd.tensor_tensor(
                    out=s_sb[u // 2][:, cols], in0=p_scaled[u][:], in1=s_sb[u // 2][:, cols], op=ALU.add
                )

        def scale_sum(u):
            if by_gpsimd(u, 1):
                cols = tile_cols(u, 1)
                nc.gpsimd.tensor_scalar(
                    out=s_sb[u // 2][:, cols], in0=s_sb[u // 2][:, cols], scalar1=C_H, scalar2=0.0, op0=ALU.mult, op1=ALU.add
                )

        def hold_gpsimd(u):
            last = tile_cols(u, 0 if by_gpsimd(u, 1) else 1).stop - 1
            probe = stream.tile([P, 1], F32, name="probe", tag="probe")
            nc.gpsimd.tensor_copy(out=probe[:], in_=s_sb[u // 2][:, last:last + 1])

        identity = const.tile([P, P], F32, name="identity", tag="identity")
        make_identity(nc, identity[:])

        x_raw = const.tile([P, 4, FEATS], BF16, name="x_raw", tag="x_raw")
        nc.sync.dma_start(
            out=x_raw[:].rearrange("p (u e) c -> p u e c", u=2), in_=x.rearrange("(u p e) c -> p u e c", u=2, e=2)
        )
        load_tiles(adj, adj_sb, "adj_sb", 0, 0, 2)
        load_tiles(adj, adj_sb, "adj_sb", 0, 2, 2)
        load_tiles(x_0, x0_sb, "x0_sb", 0, 0, 4)
        load_tiles(adj, adj_sb, "adj_sb", 1, 0, 4)
        load_tiles(x_0, x0_sb, "x0_sb", 1, 0, 4)
        load_tiles(adj, adj_sb, "adj_sb", 2, 0, 2)
        w_raw = const.tile([P, 4, FEATS], BF16, name="w_raw", tag="w_raw")
        nc.sync.dma_start(out=w_raw[:], in_=weight1.rearrange("(t p) c -> p t c", p=P))
        load_tiles(adj, adj_sb, "adj_sb", 2, 2, 2)
        load_tiles(x_0, x0_sb, "x0_sb", 2, 0, 4)
        for g in range(3, LOADS_AHEAD):
            load_chunk(g)

        x_grouped = const.tile([P, CHUNK_COLS], BF16, name="x_grouped", tag="x_grouped", align_bytes=64)
        x_dst, x_src = x_grouped[:].rearrange("p (c t) -> p c t", t=4), x_raw[:].rearrange("p t c -> p c t")
        nc.vector.tensor_copy(out=x_dst[:, :320, :], in_=x_src[:, :320, :])
        nc.scalar.copy(out=x_dst[:, 320:, :], in_=x_src[:, 320:, :])
        weights["x"] = quantise(const, x_grouped, 0, CHUNK_COLS, "x")

        w_grouped = const.tile([P, CHUNK_COLS], BF16, name="w_grouped", tag="w_grouped", align_bytes=64)

        def regroup_weight_part(q):
            cols = slice(q * P, (q + 1) * P)
            nc.gpsimd.tensor_scalar(
                out=w_grouped[:].rearrange("p (c t) -> p c t", t=4)[:, cols, :], in0=w_raw[:].rearrange("p t c -> p c t")[:, cols, :],
                scalar1=1.0, scalar2=0.0, op0=ALU.mult, op1=ALU.add,
            )

        for j in range(-3, N_UNITS + 7):
            if live(j):
                first_product(j)
            if live(j - 4):
                second_product(j - 4)
            if live(j + 1) or live(j - 3):
                quantise_step(j)
            if j == 3:
                weights["w"] = quantise(const, w_grouped, 0, CHUNK_COLS, "w")
            if live(j):
                first_sum(j)
            if live(j - 4):
                second_sum(j - 4)
            if live(j + 3):
                transpose_adj(j + 3)
            if live(j - 1):
                transpose_s(j - 1)
            if live(j + 3) or live(j - 1):
                grouped[j + 2] = stream.tile([P, CHUNK_COLS], BF16, name="grouped", tag="grouped", align_bytes=64)
            if live(j - 4):
                scale_product(j - 4)
            if live(j + 3):
                regroup_adj(j + 3)
            if live(j - 1):
                regroup_m(j - 1)
            if live(j + 3) and not by_gpsimd(j + 3, 1):
                scale_x0_scalar(j + 3)
            if live(j - 5):
                hold_gpsimd(j - 5)
            if live(j - 5):
                finish_on_gpsimd(j - 5)
            if j % 2 == 1 and live(j + 1):
                scale_x0_gpsimd((j + 1) // 2)
            if live(j - 4):
                scale_sum(j - 4)
            if 1 <= j < 3:
                regroup_weight_part(2 * j - 2)
                regroup_weight_part(2 * j - 1)
            if live(j - 6):
                store_unit(j - 6)
            if j >= 1 and j % 2 == 1 and (j - 1) // 2 + LOADS_AHEAD < N_CHUNKS:
                load_chunk((j - 1) // 2 + LOADS_AHEAD)
